import numpy as np
import ml_dtypes


def mxq(x, axis, fmt="e4m3"):
    dtype, down = {"e4m3": (ml_dtypes.float8_e4m3fn, 7), "e5m2": (ml_dtypes.float8_e5m2, 14)}[fmt]
    v = np.moveaxis(np.asarray(x, np.float32).astype(ml_dtypes.bfloat16).astype(np.float64), axis, -1)
    blocks = v.reshape(v.shape[:-1] + (-1, 32))
    amax = np.abs(blocks).max(-1, keepdims=True)
    byte = np.maximum(np.where(amax > 0, np.frexp(amax)[1] - 1 + 127, 0) - down, 1)
    scale = np.exp2(byte - 127.0)
    codes = (blocks / scale).astype(np.float32).astype(dtype).astype(np.float64)
    return np.moveaxis((codes * scale).reshape(v.shape), -1, axis)


WIDE = False


def mx_kscale(k):
    if not WIDE:
        return np.ones(k)
    levels = np.array([10, -10, 5, -5, 0])
    if k % 512:
        return np.exp2(np.random.permutation(np.resize(levels, k // 32))).repeat(32)
    a = np.empty((k // 512, 16))
    for p in range(k // 512):
        a[p, :8] = np.random.permutation(np.resize(levels, 8))
        for g in range(8):
            far = levels[np.abs(levels - a[p, g]) >= 10]
            a[p, g + 8] = far[np.random.randint(len(far))]
    return np.exp2(a.ravel()).repeat(32)


BF16 = ml_dtypes.bfloat16


def bf(x):
    return np.asarray(x, np.float32).astype(BF16)


def f64(x):
    return np.asarray(x).astype(np.float64)


N, IN, OUT, R, KD, K = 512, 2048, 2048, 32, 32, 16
KR = K * R
GATE_THRESHOLD = 0.05


def setup_inputs():
    s, t = mx_kscale(IN), mx_kscale(KR)
    tk = t.reshape(K, R)
    return {"x": bf(np.random.standard_normal((N, IN)) * s),
            "scores": bf(np.random.standard_normal((N, K))),
            "Wb": bf(np.random.standard_normal((OUT, IN)) / np.sqrt(IN) / s),
            "bb": bf(np.random.standard_normal(OUT) * 0.3),
            "A": bf(np.random.standard_normal((K, OUT, R)) * 2.0 / np.sqrt(R) / tk[:, None, :]),
            "B": bf(np.random.standard_normal((K, R, IN)) / np.sqrt(IN) / s * tk[:, :, None])}


def reference(x, scores, Wb, bb, A, B):
    xq = mxq(f64(x), 1, "e4m3")
    base = (xq @ mxq(f64(Wb), 1, "e4m3").T) + f64(bb)
    sc = f64(scores)
    e = np.exp(sc - sc.max(-1, keepdims=True))
    g = e / e.sum(-1, keepdims=True)
    g = np.where(g > GATE_THRESHOLD, g, 0.0)
    g = g / np.maximum(g.sum(-1, keepdims=True), 1e-8)
    u = xq @ mxq(f64(B).reshape(KR, IN), 1, "e4m3").T
    h = (g[:, :, None] * u.reshape(N, K, R)).reshape(N, KR)
    Af = f64(A).transpose(0, 2, 1).reshape(KR, OUT)
    delta = mxq(h, 1, "e4m3") @ mxq(Af, 0, "e4m3")
    return base + delta

@@ -1,0 +1,326 @@
+from contextlib import ExitStack
+
+import concourse.mybir as mybir
+from concourse.masks import make_identity
+
+F32 = mybir.dt.float32
+BF16 = mybir.dt.bfloat16
+U32 = mybir.dt.uint32
+U8 = mybir.dt.uint8
+FP8X4 = mybir.dt.float8_e4m3fn_x4
+ALU = mybir.AluOpType
+ACT = mybir.ActivationFunctionType
+AX = mybir.AxisListType
+
+P = 128
+N_TOK = 512
+D_IN = 2048
+D_OUT = 2048
+N_EXP = 16
+RANK = 32
+KR = N_EXP * RANK
+NB = N_TOK // P
+G = D_IN // 512
+MC = D_OUT // 512
+GATE_THRESHOLD = 0.05
+
+FLOPS = 2 * N_TOK * D_IN * D_OUT + 2 * N_TOK * D_IN * KR + 2 * N_TOK * KR * D_OUT
+
+
+PIN = True
+
+
+def tile_submatrixlinear_pa_kernel(tc, x, scores, Wb, bb, A, B, out):
+    nc = tc.nc
+    with ExitStack() as ctx:
+        const = ctx.enter_context(tc.tile_pool(name="const", bufs=1))
+        raw = ctx.enter_context(tc.tile_pool(name="raw", bufs=12))
+        grp = ctx.enter_context(tc.tile_pool(name="grp", bufs=3))
+        outp = ctx.enter_context(tc.tile_pool(name="outp", bufs=6))
+        small = ctx.enter_context(tc.tile_pool(name="small", bufs=1))
+        tps = ctx.enter_context(tc.psum_pool(name="tps", bufs=4))
+        accs = ctx.enter_context(tc.psum_pool(name="accs", bufs=4))
+        if PIN:
+            ctx.enter_context(tc.manual_schedule())
+
+        ident = const.tile([P, P], F32, name="ident")
+        make_identity(nc, ident[:])
+        ones = const.tile([P, P], BF16, name="ones")
+        nc.vector.memset(ones[:], 1.0)
+        bias_row = raw.tile([P, D_OUT], BF16, name="bias_row", tag="raw")
+        nc.vector.memset(bias_row[:], 0.0)
+
+        bias_sb = const.tile([P, D_OUT], F32, name="bias_sb")
+        z0 = [const.tile([P, N_EXP, 256], BF16, name="z0_%d" % a) for a in range(MC // 2)]
+        gt = const.tile([P, NB, P], F32, name="gt")
+        xq = const.tile([P, NB, G, P], U32, name="xq", align_bytes=64)
+        xs = const.tile([P, NB, G, P], U8, name="xs", align_bytes=64)
+        bq = const.tile([P, 4, G, P], U32, name="bq", align_bytes=64)
+        bs = const.tile([P, 4, G, P], U8, name="bs", align_bytes=64)
+        wq = const.tile([P, MC, G, 512], U32, name="wq", align_bytes=64)
+        ws = const.tile([P, MC, G, 512], U8, name="ws", align_bytes=64)
+        aq = const.tile([P, MC, 512], U32, name="aq", align_bytes=64)
+        asc = const.tile([P, MC, 512], U8, name="asc", align_bytes=64)
+        hq = const.tile([P, NB, P], U32, name="hq", align_bytes=64)
+        hs = const.tile([P, NB, P], U8, name="hs", align_bytes=64)
+        hg = const.tile([P, NB, P, 4], BF16, name="hg", align_bytes=64)
+
+        xv = x.rearrange("(p c) i -> c p i", c=NB)
+        outv = out.rearrange("(p c) o -> c p o", c=NB)
+        Bv = B.rearrange("k r i -> (k r) i").rearrange("(p t) i -> t p i", t=4)
+        sc_b = small.tile([P, NB, N_EXP], BF16, name="sc_b")
+        nc.sync.dma_start(out=sc_b[:], in_=scores.rearrange("(p c) k -> p c k", c=NB))
+        nc.sync.dma_start(out=bias_row[0:1, :], in_=bb.rearrange("(o n) -> o n", o=1))
+
+        def load_rows(src, nm):
+            t = raw.tile([P, D_IN], BF16, name=nm, tag="raw")
+            nc.sync.dma_start(out=t[:], in_=src)
+            return t
+
+        def load_a(m):
+            nc.sync.dma_start(
+                out=z0[m][:],
+                in_=A[:, 1024 * m : 1024 * m + 1024, :].rearrange("k (w b) r -> w k (b r)", b=8),
+            )
+
+        x_raw = [load_rows(xv[c], "x_raw") for c in range(NB)]
+        b_raw = [load_rows(Bv[t], "b_raw") for t in range(4)]
+        w_raw = []
+        for m in range(MC):
+            for j in range(4):
+                r0 = 512 * m + P * j
+                w_raw.append(load_rows(Wb[r0 : r0 + P, :], "w_raw"))
+            if m % 2 == 0:
+                load_a(m // 2)
+
+        mx = small.tile([P, NB], F32, name="mx")
+        nc.vector.tensor_reduce(out=mx[:], in_=sc_b[:], axis=AX.X, op=ALU.max)
+        dif = small.tile([P, NB, N_EXP], F32, name="dif")
+        nc.vector.tensor_tensor(
+            out=dif[:], in0=sc_b[:], in1=mx[:].unsqueeze(2).to_broadcast([P, NB, N_EXP]), op=ALU.subtract
+        )
+        ex = small.tile([P, NB, N_EXP], F32, name="ex")
+        nc.scalar.activation(out=ex[:], in_=dif[:], func=ACT.Exp)
+        sm = small.tile([P, NB], F32, name="sm")
+        nc.vector.tensor_reduce(out=sm[:], in_=ex[:], axis=AX.X, op=ALU.add)
+        rs = small.tile([P, NB], F32, name="rs")
+        nc.vector.reciprocal(out=rs[:], in_=sm[:])
+        g0 = small.tile([P, NB, N_EXP], F32, name="g0")
+        nc.vector.tensor_tensor(
+            out=g0[:], in0=ex[:], in1=rs[:].unsqueeze(2).to_broadcast([P, NB, N_EXP]), op=ALU.mult
+        )
+        g1 = small.tile([P, NB, N_EXP], F32, name="g1")
+        nc.vector.scalar_tensor_tensor(
+            out=g1[:].rearrange("p c k -> p (c k)"),
+            in0=g0[:].rearrange("p c k -> p (c k)"),
+            scalar=GATE_THRESHOLD,
+            in1=g0[:].rearrange("p c k -> p (c k)"),
+            op0=ALU.is_gt,
+            op1=ALU.mult,
+        )
+        s1 = small.tile([P, NB], F32, name="s1")
+        nc.vector.tensor_reduce(out=s1[:], in_=g1[:], axis=AX.X, op=ALU.add)
+        s1m = small.tile([P, NB], F32, name="s1m")
+        nc.vector.tensor_scalar_max(out=s1m[:], in0=s1[:], scalar1=1e-8)
+        r1 = small.tile([P, NB], F32, name="r1")
+        nc.vector.reciprocal(out=r1[:], in_=s1m[:])
+        gexps = []
+        for nb in range(NB):
+            gexp = outp.tile([P, 512], F32, name="gexp", tag="o")
+            nc.vector.tensor_scalar(
+                out=gexp[:, 0:P].rearrange("p (k j) -> p k j", j=8),
+                in0=g1[:, nb, :].unsqueeze(2).to_broadcast([P, N_EXP, 8]),
+                scalar1=r1[:, nb : nb + 1],
+                scalar2=None,
+                op0=ALU.mult,
+            )
+            gexps.append(gexp)
+
+        for m in range(MC):
+            pb = accs.tile([P, 512], F32, name="pb", tag="acc")
+            nc.tensor.matmul(out=pb[:], lhsT=ones[:], rhs=bias_row[:, 512 * m : 512 * m + 512], start=True, stop=True)
+            nc.scalar.copy(out=bias_sb[:, 512 * m : 512 * m + 512], in_=pb[:])
+
+        def transpose_rows(src, dst):
+            words = src[:].bitcast(F32)
+            for gp in range(2):
+                bank = tps.tile([P, 4, P], F32, name="bank", tag="tp")
+                for g2 in range(2):
+                    for u in range(2):
+                        c0 = 256 * (2 * gp + g2)
+                        nc.tensor.transpose(bank[:, 2 * g2 + u, :], words[:, c0 + u : c0 + 256 : 2], ident[:])
+                if gp == 0:
+                    nc.scalar.copy(
+                        out=dst[:, 2 * gp : 2 * gp + 2],
+                        in_=bank[:].rearrange("p (g u) n -> p g n u", u=2),
+                    )
+                else:
+                    nc.vector.tensor_copy(
+                        out=dst[:, 2 * gp : 2 * gp + 2],
+                        in_=bank[:].rearrange("p (g u) n -> p g n u", u=2),
+                    )
+
+        def rows_to_codes(src, codes, scales):
+            gx = grp.tile([P, 2048], BF16, name="gx", tag="gx", align_bytes=64)
+            transpose_rows(src, gx[:].bitcast(F32).rearrange("p (g n u) -> p g n u", g=G, n=P, u=2))
+            nc.vector.quantize_mx(
+                out=codes.rearrange("p g n -> p (g n)").bitcast(FP8X4),
+                scales=scales.rearrange("p g n -> p (g n)"),
+                in_=gx[:],
+            )
+
+        def ut_passes(ut, t, nb):
+            for g in range(G):
+                nc.tensor.matmul_mx(
+                    out=ut[nb][:, t, :],
+                    lhsT=bq[:, t, g, :].bitcast(FP8X4),
+                    lhsT_scale=bs[:, t, g, :],
+                    rhs=xq[:, nb, g, :].bitcast(FP8X4),
+                    rhs_scale=xs[:, nb, g, :],
+                    start=(g == 0),
+                    stop=(g == G - 1),
+                )
+
+        def a_sort(m):
+            z1 = grp.tile([P, 4096], BF16, name="z1", tag="z1", bufs=1)
+            zo = z1[:].bitcast(F32).rearrange("p (b u k j) -> p u b k j", b=8, u=2, k=N_EXP, j=8)
+            zi = z0[m][:].rearrange("p k c -> p (k c)").bitcast(F32).rearrange("p (k b j u) -> p u b k j", k=N_EXP, b=8, j=8, u=2)
+            for u in range(2):
+                nc.scalar.copy(out=zo[:, u], in_=zi[:, u])
+            return z1
+
+        def a_transposes(m, z1):
+            y = grp.tile([P, 4096], BF16, name="y", tag="y", bufs=1, align_bytes=64)
+            yw = y[:].bitcast(F32).rearrange("p (w h bu) -> p h w bu", w=P, h=4, bu=4)
+            zw = z1[:].bitcast(F32)
+            for h in range(4):
+                bank = tps.tile([P, 4, P], F32, name="bank", tag="tp")
+                for b in range(4):
+                    c0 = P * (4 * h + b)
+                    nc.tensor.transpose(bank[:, b, :], zw[:, c0 : c0 + P], ident[:])
+                nc.scalar.copy(out=yw[:, h], in_=bank[:].rearrange("p bu w -> p w bu"))
+            return y
+
+        def a_quantise(m, y):
+            for i in range(2):
+                nc.vector.quantize_mx(
+                    out=aq[:, 2 * m + i, :].bitcast(FP8X4), scales=asc[:, 2 * m + i, :], in_=y[:, 2048 * i : 2048 * i + 2048]
+                )
+
+        def w_half(m, half, wg):
+            wgw = wg[:].bitcast(F32).rearrange("p (g j n u) -> p j g n u", g=G, j=4, n=P, u=2)
+            for j in (2 * half, 2 * half + 1):
+                transpose_rows(w_raw[4 * m + j], wgw[:, j])
+
+        def w_quantise(m, wg):
+            for g in range(G):
+                nc.vector.quantize_mx(
+                    out=wq[:, m, g, :].bitcast(FP8X4), scales=ws[:, m, g, :], in_=wg[:, 2048 * g : 2048 * g + 2048]
+                )
+
+        def w_tile():
+            wg = grp.tile([P, G * 2048], BF16, name="wg", tag="wg", bufs=2, align_bytes=64)
+            return wg
+
+        def base(m, nb):
+            acc = accs.tile([P, 512], F32, name="acc", tag="acc")
+            for g in range(G):
+                nc.tensor.matmul_mx(
+                    out=acc[:],
+                    lhsT=xq[:, nb, g, :].bitcast(FP8X4),
+                    lhsT_scale=xs[:, nb, g, :],
+                    rhs=wq[:, m, g, :].bitcast(FP8X4),
+                    rhs_scale=ws[:, m, g, :],
+                    start=(g == 0),
+                    stop=False,
+                )
+            return acc
+
+        def delta(m, nb, acc):
+            nc.tensor.matmul_mx(
+                out=acc[:],
+                lhsT=hq[:, nb, :].bitcast(FP8X4),
+                lhsT_scale=hs[:, nb, :],
+                rhs=aq[:, m, :].bitcast(FP8X4),
+                rhs_scale=asc[:, m, :],
+                start=False,
+                stop=True,
+            )
+
+        def finish(m, nb, acc):
+            o = outp.tile([P, 512], F32, name="o", tag="o")
+            nc.vector.tensor_tensor(out=o[:], in0=acc[:], in1=bias_sb[:, 512 * m : 512 * m + 512], op=ALU.add)
+            nc.sync.dma_start(out=outv[nb][:, 512 * m : 512 * m + 512], in_=o[:])
+
+        def h_block(nb):
+            nc.vector.tensor_tensor(
+                out=hg[:, nb],
+                in0=ut[nb][:].rearrange("p t n -> p n t"),
+                in1=gt[:, nb].unsqueeze(2).to_broadcast([P, P, 4]),
+                op=ALU.mult,
+            )
+
+        for nb in range(NB):
+            rows_to_codes(x_raw[nb], xq[:, nb], xs[:, nb])
+
+        bank = tps.tile([P, 4, P], F32, name="bank", tag="tp")
+        for c in range(NB):
+            nc.tensor.transpose(bank[:, c, :], gexps[c][:, 0:P], ident[:])
+        nc.scalar.copy(out=gt[:], in_=bank[:])
+
+        for t in range(3):
+            rows_to_codes(b_raw[t], bq[:, t], bs[:, t])
+        ut = [accs.tile([P, 4, P], F32, name="ut%d" % nb, tag="acc") for nb in range(NB)]
+        for nb in range(NB):
+            ut_passes(ut, 0, nb)
+        rows_to_codes(b_raw[3], bq[:, 3], bs[:, 3])
+        for nb in range(NB):
+            ut_passes(ut, 1, nb)
+        wg = w_tile()
+        w_half(0, 0, wg)
+        for nb in range(NB):
+            ut_passes(ut, 2, nb)
+        w_half(0, 1, wg)
+        z1 = a_sort(0)
+        for nb in range(NB):
+            ut_passes(ut, 3, nb)
+        y = a_transposes(0, z1)
+        h_block(0)
+        w_quantise(0, wg)
+        for nb in range(1, NB):
+            h_block(nb)
+        a_quantise(0, y)
+        nc.vector.quantize_mx(
+            out=hq[:].rearrange("p c n -> p (c n)").bitcast(FP8X4),
+            scales=hs[:].rearrange("p c n -> p (c n)"),
+            in_=hg[:].rearrange("p c n t -> p (c n t)"),
+        )
+
+        late = []
+        for m in range(MC - 1):
+            wg = w_tile()
+            w_half(m + 1, 0, wg)
+            for nb, acc in late:
+                finish(m - 1, nb, acc)
+            accl = [base(m, 0), base(m, 1)]
+            w_half(m + 1, 1, wg)
+            accl.append(base(m, 2))
+            accl.append(base(m, 3))
+            if m == 1:
+                z1 = a_sort(1)
+                y = a_transposes(1, z1)
+            for nb in range(NB):
+                delta(m, nb, accl[nb])
+            w_quantise(m + 1, wg)
+            if m == 1:
+                a_quantise(1, y)
+            finish(m, 0, accl[0])
+            finish(m, 1, accl[1])
+            late = [(2, accl[2]), (3, accl[3])]
+
+        for nb, acc in late:
+            finish(MC - 2, nb, acc)
+        for nb in range(NB):
+            acc = base(MC - 1, nb)
+            delta(MC - 1, nb, acc)
+            finish(MC - 1, nb, acc)

@@ -27,31 +27,18 @@ GATE_THRESHOLD = 0.05
 FLOPS = 2 * N_TOK * D_IN * D_OUT + 2 * N_TOK * D_IN * KR + 2 * N_TOK * KR * D_OUT
 
 
-PIN = True
-
-
 def tile_submatrixlinear_pa_kernel(tc, x, scores, Wb, bb, A, B, out):
     nc = tc.nc
     with ExitStack() as ctx:
         const = ctx.enter_context(tc.tile_pool(name="const", bufs=1))
-        raw = ctx.enter_context(tc.tile_pool(name="raw", bufs=12))
-        grp = ctx.enter_context(tc.tile_pool(name="grp", bufs=3))
-        outp = ctx.enter_context(tc.tile_pool(name="outp", bufs=6))
-        small = ctx.enter_context(tc.tile_pool(name="small", bufs=1))
+        raw = ctx.enter_context(tc.tile_pool(name="raw", bufs=11))
+        work = ctx.enter_context(tc.tile_pool(name="work", bufs=3))
+        outp = ctx.enter_context(tc.tile_pool(name="outp", bufs=4))
         tps = ctx.enter_context(tc.psum_pool(name="tps", bufs=4))
         accs = ctx.enter_context(tc.psum_pool(name="accs", bufs=4))
-        if PIN:
-            ctx.enter_context(tc.manual_schedule())
-
-        ident = const.tile([P, P], F32, name="ident")
-        make_identity(nc, ident[:])
-        ones = const.tile([P, P], BF16, name="ones")
-        nc.vector.memset(ones[:], 1.0)
-        bias_row = raw.tile([P, D_OUT], BF16, name="bias_row", tag="raw")
-        nc.vector.memset(bias_row[:], 0.0)
+        ctx.enter_context(tc.manual_schedule())
 
         bias_sb = const.tile([P, D_OUT], F32, name="bias_sb")
-        z0 = [const.tile([P, N_EXP, 256], BF16, name="z0_%d" % a) for a in range(MC // 2)]
         gt = const.tile([P, NB, P], F32, name="gt")
         xq = const.tile([P, NB, G, P], U32, name="xq", align_bytes=64)
         xs = const.tile([P, NB, G, P], U8, name="xs", align_bytes=64)
@@ -59,8 +46,8 @@ def tile_submatrixlinear_pa_kernel(tc, x, scores, Wb, bb, A, B, out):
         bs = const.tile([P, 4, G, P], U8, name="bs", align_bytes=64)
         wq = const.tile([P, MC, G, 512], U32, name="wq", align_bytes=64)
         ws = const.tile([P, MC, G, 512], U8, name="ws", align_bytes=64)
-        aq = const.tile([P, MC, 512], U32, name="aq", align_bytes=64)
-        asc = const.tile([P, MC, 512], U8, name="asc", align_bytes=64)
+        aq = const.tile([P, D_OUT], U32, name="aq", align_bytes=64)
+        asc = const.tile([P, D_OUT], U8, name="asc", align_bytes=64)
         hq = const.tile([P, NB, P], U32, name="hq", align_bytes=64)
         hs = const.tile([P, NB, P], U8, name="hs", align_bytes=64)
         hg = const.tile([P, NB, P, 4], BF16, name="hg", align_bytes=64)
@@ -68,48 +55,59 @@ def tile_submatrixlinear_pa_kernel(tc, x, scores, Wb, bb, A, B, out):
         xv = x.rearrange("(p c) i -> c p i", c=NB)
         outv = out.rearrange("(p c) o -> c p o", c=NB)
         Bv = B.rearrange("k r i -> (k r) i").rearrange("(p t) i -> t p i", t=4)
-        sc_b = small.tile([P, NB, N_EXP], BF16, name="sc_b")
-        nc.sync.dma_start(out=sc_b[:], in_=scores.rearrange("(p c) k -> p c k", c=NB))
-        nc.sync.dma_start(out=bias_row[0:1, :], in_=bb.rearrange("(o n) -> o n", o=1))
 
-        def load_rows(src, nm):
-            t = raw.tile([P, D_IN], BF16, name=nm, tag="raw")
-            nc.sync.dma_start(out=t[:], in_=src)
+        sc_b = const.tile([P, NB, N_EXP], BF16, name="sc_b")
+        nc.scalar.dma_start(out=sc_b[:], in_=scores.rearrange("(p c) k -> p c k", c=NB))
+        bias_row = const.tile([P, D_OUT], BF16, name="bias_row")
+
+        def load_rows(src, cuts=1):
+            t = raw.tile([P, D_IN], BF16, name="rows", tag="raw")
+            step = D_IN // cuts
+            for c in range(cuts):
+                nc.sync.dma_start(out=t[:, step * c : step * c + step], in_=src[:, step * c : step * c + step])
             return t
 
-        def load_a(m):
+        def load_a(half):
+            z = const.tile([P, N_EXP, 256], BF16, name="z0_%d" % half)
             nc.sync.dma_start(
-                out=z0[m][:],
-                in_=A[:, 1024 * m : 1024 * m + 1024, :].rearrange("k (w b) r -> w k (b r)", b=8),
+                out=z[:], in_=A[:, 1024 * half : 1024 * half + 1024, :].rearrange("k (w b) r -> w k (b r)", b=8)
             )
+            return z
 
-        x_raw = [load_rows(xv[c], "x_raw") for c in range(NB)]
-        b_raw = [load_rows(Bv[t], "b_raw") for t in range(4)]
+        nc.gpsimd.memset(bias_row[:].bitcast(F32), 0.0)
+        ident = const.tile([P, P], F32, name="ident")
+        make_identity(nc, ident[:])
+        ones = const.tile([P, P], BF16, name="ones")
+        nc.vector.memset(ones[:], 1.0)
+
+        x_raw = [load_rows(xv[c], 2 if c == 0 else 1) for c in range(NB)]
+        nc.sync.dma_start(out=bias_row[0:1, :], in_=bb.rearrange("(o n) -> o n", o=1))
+        b_raw = [load_rows(Bv[t]) for t in range(4)]
         w_raw = []
+        z0 = []
         for m in range(MC):
             for j in range(4):
-                r0 = 512 * m + P * j
-                w_raw.append(load_rows(Wb[r0 : r0 + P, :], "w_raw"))
-            if m % 2 == 0:
-                load_a(m // 2)
+                w_raw.append(load_rows(Wb[512 * m + P * j : 512 * m + P * j + P, :]))
+            if m < 2:
+                z0.append(load_a(m))
 
-        mx = small.tile([P, NB], F32, name="mx")
+        mx = const.tile([P, NB], F32, name="mx")
         nc.vector.tensor_reduce(out=mx[:], in_=sc_b[:], axis=AX.X, op=ALU.max)
-        dif = small.tile([P, NB, N_EXP], F32, name="dif")
+        dif = const.tile([P, NB, N_EXP], F32, name="dif")
         nc.vector.tensor_tensor(
             out=dif[:], in0=sc_b[:], in1=mx[:].unsqueeze(2).to_broadcast([P, NB, N_EXP]), op=ALU.subtract
         )
-        ex = small.tile([P, NB, N_EXP], F32, name="ex")
+        ex = const.tile([P, NB, N_EXP], F32, name="ex")
         nc.scalar.activation(out=ex[:], in_=dif[:], func=ACT.Exp)
-        sm = small.tile([P, NB], F32, name="sm")
+        sm = const.tile([P, NB], F32, name="sm")
         nc.vector.tensor_reduce(out=sm[:], in_=ex[:], axis=AX.X, op=ALU.add)
-        rs = small.tile([P, NB], F32, name="rs")
+        rs = const.tile([P, NB], F32, name="rs")
         nc.vector.reciprocal(out=rs[:], in_=sm[:])
-        g0 = small.tile([P, NB, N_EXP], F32, name="g0")
+        g0 = const.tile([P, NB, N_EXP], F32, name="g0")
         nc.vector.tensor_tensor(
             out=g0[:], in0=ex[:], in1=rs[:].unsqueeze(2).to_broadcast([P, NB, N_EXP]), op=ALU.mult
         )
-        g1 = small.tile([P, NB, N_EXP], F32, name="g1")
+        g1 = const.tile([P, NB, N_EXP], F32, name="g1")
         nc.vector.scalar_tensor_tensor(
             out=g1[:].rearrange("p c k -> p (c k)"),
             in0=g0[:].rearrange("p c k -> p (c k)"),
@@ -118,139 +116,69 @@ def tile_submatrixlinear_pa_kernel(tc, x, scores, Wb, bb, A, B, out):
             op0=ALU.is_gt,
             op1=ALU.mult,
         )
-        s1 = small.tile([P, NB], F32, name="s1")
+        s1 = const.tile([P, NB], F32, name="s1")
         nc.vector.tensor_reduce(out=s1[:], in_=g1[:], axis=AX.X, op=ALU.add)
-        s1m = small.tile([P, NB], F32, name="s1m")
+        s1m = const.tile([P, NB], F32, name="s1m")
         nc.vector.tensor_scalar_max(out=s1m[:], in0=s1[:], scalar1=1e-8)
-        r1 = small.tile([P, NB], F32, name="r1")
+        r1 = const.tile([P, NB], F32, name="r1")
         nc.vector.reciprocal(out=r1[:], in_=s1m[:])
-        gexps = []
+        gexp = const.tile([P, NB, P], F32, name="gexp")
         for nb in range(NB):
-            gexp = outp.tile([P, 512], F32, name="gexp", tag="o")
-            nc.vector.tensor_scalar(
-                out=gexp[:, 0:P].rearrange("p (k j) -> p k j", j=8),
+            nc.gpsimd.tensor_scalar(
+                out=gexp[:, nb, :].rearrange("p (k j) -> p k j", j=8),
                 in0=g1[:, nb, :].unsqueeze(2).to_broadcast([P, N_EXP, 8]),
                 scalar1=r1[:, nb : nb + 1],
-                scalar2=None,
+                scalar2=0.0,
                 op0=ALU.mult,
+                op1=ALU.add,
             )
-            gexps.append(gexp)
 
-        for m in range(MC):
-            pb = accs.tile([P, 512], F32, name="pb", tag="acc")
-            nc.tensor.matmul(out=pb[:], lhsT=ones[:], rhs=bias_row[:, 512 * m : 512 * m + 512], start=True, stop=True)
-            nc.scalar.copy(out=bias_sb[:, 512 * m : 512 * m + 512], in_=pb[:])
+        def psum_bank():
+            bank = tps.tile([P, 4, P], F32, name="bank", tag="tp")
+            return bank
 
-        def transpose_rows(src, dst):
+        def part(src):
+            t = work.tile([P, D_IN], BF16, name="parted", tag="parted", bufs=4)
+            nc.vector.tensor_copy(
+                out=t[:].bitcast(F32).rearrange("q (g u p) -> q g u p", g=G, u=2),
+                in_=src[:].bitcast(F32).rearrange("q (g p u) -> q g u p", g=G, u=2),
+            )
+            return t
+
+        def turn_block(src, parted, second):
+            gx = work.tile([P, D_IN], BF16, name="gx", tag="gx", align_bytes=64)
+            dst = gx[:].bitcast(F32).rearrange("p (g n u) -> p g n u", g=G, u=2)
             words = src[:].bitcast(F32)
             for gp in range(2):
-                bank = tps.tile([P, 4, P], F32, name="bank", tag="tp")
+                bank = psum_bank()
                 for g2 in range(2):
                     for u in range(2):
                         c0 = 256 * (2 * gp + g2)
-                        nc.tensor.transpose(bank[:, 2 * g2 + u, :], words[:, c0 + u : c0 + 256 : 2], ident[:])
-                if gp == 0:
-                    nc.scalar.copy(
-                        out=dst[:, 2 * gp : 2 * gp + 2],
-                        in_=bank[:].rearrange("p (g u) n -> p g n u", u=2),
-                    )
-                else:
-                    nc.vector.tensor_copy(
-                        out=dst[:, 2 * gp : 2 * gp + 2],
-                        in_=bank[:].rearrange("p (g u) n -> p g n u", u=2),
-                    )
+                        cols = slice(c0 + P * u, c0 + P * u + P) if parted else slice(c0 + u, c0 + 256, 2)
+                        nc.tensor.transpose(bank[:, 2 * g2 + u, :], words[:, cols], ident[:])
+                copy = nc.scalar.copy if gp == 0 else second
+                copy(out=dst[:, 2 * gp : 2 * gp + 2], in_=bank[:].rearrange("p (g u) n -> p g n u", u=2))
+            return gx
 
-        def rows_to_codes(src, codes, scales):
-            gx = grp.tile([P, 2048], BF16, name="gx", tag="gx", align_bytes=64)
-            transpose_rows(src, gx[:].bitcast(F32).rearrange("p (g n u) -> p g n u", g=G, n=P, u=2))
+        def quantise_block(gx, codes, scales):
             nc.vector.quantize_mx(
                 out=codes.rearrange("p g n -> p (g n)").bitcast(FP8X4),
                 scales=scales.rearrange("p g n -> p (g n)"),
                 in_=gx[:],
             )
 
-        def ut_passes(ut, t, nb):
-            for g in range(G):
-                nc.tensor.matmul_mx(
-                    out=ut[nb][:, t, :],
-                    lhsT=bq[:, t, g, :].bitcast(FP8X4),
-                    lhsT_scale=bs[:, t, g, :],
-                    rhs=xq[:, nb, g, :].bitcast(FP8X4),
-                    rhs_scale=xs[:, nb, g, :],
-                    start=(g == 0),
-                    stop=(g == G - 1),
-                )
-
-        def a_sort(m):
-            z1 = grp.tile([P, 4096], BF16, name="z1", tag="z1", bufs=1)
-            zo = z1[:].bitcast(F32).rearrange("p (b u k j) -> p u b k j", b=8, u=2, k=N_EXP, j=8)
-            zi = z0[m][:].rearrange("p k c -> p (k c)").bitcast(F32).rearrange("p (k b j u) -> p u b k j", k=N_EXP, b=8, j=8, u=2)
-            for u in range(2):
-                nc.scalar.copy(out=zo[:, u], in_=zi[:, u])
-            return z1
-
-        def a_transposes(m, z1):
-            y = grp.tile([P, 4096], BF16, name="y", tag="y", bufs=1, align_bytes=64)
-            yw = y[:].bitcast(F32).rearrange("p (w h bu) -> p h w bu", w=P, h=4, bu=4)
-            zw = z1[:].bitcast(F32)
-            for h in range(4):
-                bank = tps.tile([P, 4, P], F32, name="bank", tag="tp")
-                for b in range(4):
-                    c0 = P * (4 * h + b)
-                    nc.tensor.transpose(bank[:, b, :], zw[:, c0 : c0 + P], ident[:])
-                nc.scalar.copy(out=yw[:, h], in_=bank[:].rearrange("p bu w -> p w bu"))
-            return y
-
-        def a_quantise(m, y):
-            for i in range(2):
-                nc.vector.quantize_mx(
-                    out=aq[:, 2 * m + i, :].bitcast(FP8X4), scales=asc[:, 2 * m + i, :], in_=y[:, 2048 * i : 2048 * i + 2048]
-                )
-
-        def w_half(m, half, wg):
-            wgw = wg[:].bitcast(F32).rearrange("p (g j n u) -> p j g n u", g=G, j=4, n=P, u=2)
-            for j in (2 * half, 2 * half + 1):
-                transpose_rows(w_raw[4 * m + j], wgw[:, j])
-
-        def w_quantise(m, wg):
-            for g in range(G):
-                nc.vector.quantize_mx(
-                    out=wq[:, m, g, :].bitcast(FP8X4), scales=ws[:, m, g, :], in_=wg[:, 2048 * g : 2048 * g + 2048]
-                )
-
-        def w_tile():
-            wg = grp.tile([P, G * 2048], BF16, name="wg", tag="wg", bufs=2, align_bytes=64)
-            return wg
-
-        def base(m, nb):
-            acc = accs.tile([P, 512], F32, name="acc", tag="acc")
-            for g in range(G):
-                nc.tensor.matmul_mx(
-                    out=acc[:],
-                    lhsT=xq[:, nb, g, :].bitcast(FP8X4),
-                    lhsT_scale=xs[:, nb, g, :],
-                    rhs=wq[:, m, g, :].bitcast(FP8X4),
-                    rhs_scale=ws[:, m, g, :],
-                    start=(g == 0),
-                    stop=False,
-                )
-            return acc
-
-        def delta(m, nb, acc):
-            nc.tensor.matmul_mx(
-                out=acc[:],
-                lhsT=hq[:, nb, :].bitcast(FP8X4),
-                lhsT_scale=hs[:, nb, :],
-                rhs=aq[:, m, :].bitcast(FP8X4),
-                rhs_scale=asc[:, m, :],
-                start=False,
-                stop=True,
-            )
-
-        def finish(m, nb, acc):
-            o = outp.tile([P, 512], F32, name="o", tag="o")
-            nc.vector.tensor_tensor(out=o[:], in0=acc[:], in1=bias_sb[:, 512 * m : 512 * m + 512], op=ALU.add)
-            nc.sync.dma_start(out=outv[nb][:, 512 * m : 512 * m + 512], in_=o[:])
+        def ut_passes(t):
+            for nb in range(NB):
+                for g in range(G):
+                    nc.tensor.matmul_mx(
+                        out=ut[nb][:, t, :],
+                        lhsT=bq[:, t, g, :].bitcast(FP8X4),
+                        lhsT_scale=bs[:, t, g, :],
+                        rhs=xq[:, nb, g, :].bitcast(FP8X4),
+                        rhs_scale=xs[:, nb, g, :],
+                        start=(g == 0),
+                        stop=(g == G - 1),
+                    )
 
         def h_block(nb):
             nc.vector.tensor_tensor(
@@ -260,67 +188,206 @@ def tile_submatrixlinear_pa_kernel(tc, x, scores, Wb, bb, A, B, out):
                 op=ALU.mult,
             )
 
-        for nb in range(NB):
-            rows_to_codes(x_raw[nb], xq[:, nb], xs[:, nb])
+        def turn_half(pair):
+            wg = work.tile([P, 2 * D_IN], BF16, name="wg", tag="wg", align_bytes=64)
+            dst = wg[:].bitcast(F32).rearrange("p (g j n u) -> p g j n u", g=G, j=2, u=2)
+            for g in range(G):
+                bank = psum_bank()
+                for j in range(2):
+                    for u in range(2):
+                        c0 = 256 * g + P * u
+                        nc.tensor.transpose(bank[:, 2 * j + u, :], pair[j][:].bitcast(F32)[:, c0 : c0 + P], ident[:])
+                nc.scalar.copy(out=dst[:, g], in_=bank[:].rearrange("p (j u) n -> p j n u", u=2))
+            return wg
 
-        bank = tps.tile([P, 4, P], F32, name="bank", tag="tp")
+        def quantise_half(s, wg):
+            m, c0 = s // 2, 256 * (s % 2)
+            for g in range(G):
+                nc.vector.quantize_mx(
+                    out=wq[:, m, g, c0 : c0 + 256].bitcast(FP8X4),
+                    scales=ws[:, m, g, c0 : c0 + 256],
+                    in_=wg[:, 1024 * g : 1024 * g + 1024],
+                )
+
+        def part_half(s):
+            return [part(w_raw[2 * s]), part(w_raw[2 * s + 1])]
+
+        def sort_a(half):
+            z1 = work.tile([P, 4096], BF16, name="z1", tag="z1", bufs=1)
+            zo = z1[:].bitcast(F32).rearrange("p (b u k j) -> p u b k j", b=8, u=2, k=N_EXP)
+            zi = z0[half][:].rearrange("p k c -> p (k c)").bitcast(F32)
+            zi = zi.rearrange("p (k b j u) -> p u b k j", k=N_EXP, b=8, u=2)
+            nc.scalar.copy(out=zo[:, 0], in_=zi[:, 0])
+            nc.vector.tensor_copy(out=zo[:, 1], in_=zi[:, 1])
+            return z1
+
+        def turn_a(z1):
+            y = work.tile([P, 4096], BF16, name="y", tag="y", bufs=1, align_bytes=64)
+            yw = y[:].bitcast(F32).rearrange("p (w h bu) -> p h w bu", w=P, h=4)
+            zw = z1[:].bitcast(F32)
+            for h in range(4):
+                bank = psum_bank()
+                for i in range(4):
+                    c0 = P * (4 * h + i)
+                    nc.tensor.transpose(bank[:, i, :], zw[:, c0 : c0 + P], ident[:])
+                nc.scalar.copy(out=yw[:, h], in_=bank[:].rearrange("p bu w -> p w bu"))
+            return y
+
+        def quantise_a(half, y):
+            for i in range(2):
+                c0 = 1024 * half + 512 * i
+                nc.vector.quantize_mx(
+                    out=aq[:, c0 : c0 + 512].bitcast(FP8X4),
+                    scales=asc[:, c0 : c0 + 512],
+                    in_=y[:, 2048 * i : 2048 * i + 2048],
+                )
+
+        acc = {}
+
+        def base(m, nb):
+            t = accs.tile([P, 512], F32, name="acc", tag="acc")
+            for g in range(G):
+                nc.tensor.matmul_mx(
+                    out=t[:],
+                    lhsT=xq[:, nb, g, :].bitcast(FP8X4),
+                    lhsT_scale=xs[:, nb, g, :],
+                    rhs=wq[:, m, g, :].bitcast(FP8X4),
+                    rhs_scale=ws[:, m, g, :],
+                    start=(g == 0),
+                    stop=False,
+                )
+            acc[m, nb] = t
+
+        def delta(m, nb):
+            nc.tensor.matmul_mx(
+                out=acc[m, nb][:],
+                lhsT=hq[:, nb, :].bitcast(FP8X4),
+                lhsT_scale=hs[:, nb, :],
+                rhs=aq[:, 512 * m : 512 * m + 512].bitcast(FP8X4),
+                rhs_scale=asc[:, 512 * m : 512 * m + 512],
+                start=False,
+                stop=True,
+            )
+
+        def group(m, nb):
+            base(m, nb)
+            delta(m, nb)
+
+        def finish(m, nb):
+            o = outp.tile([P, 512], F32, name="o", tag="o")
+            nc.vector.tensor_tensor(
+                out=o[:], in0=acc[m, nb][:], in1=bias_sb[:, 512 * m : 512 * m + 512], op=ALU.add
+            )
+            nc.sync.dma_start(out=outv[nb][:, 512 * m : 512 * m + 512], in_=o[:])
+
+        gx0 = turn_block(x_raw[0], False, nc.vector.tensor_copy)
+        gx1 = turn_block(x_raw[1], False, nc.vector.tensor_copy)
+        quantise_block(gx0, xq[:, 0], xs[:, 0])
+        gx2 = turn_block(x_raw[2], False, nc.vector.tensor_copy)
+        quantise_block(gx1, xq[:, 1], xs[:, 1])
+        gx3 = turn_block(x_raw[3], False, nc.vector.tensor_copy)
+        quantise_block(gx2, xq[:, 2], xs[:, 2])
+        p0 = part(b_raw[0])
+        quantise_block(gx3, xq[:, 3], xs[:, 3])
+        p1 = part(b_raw[1])
+
+        gbank = psum_bank()
         for c in range(NB):
-            nc.tensor.transpose(bank[:, c, :], gexps[c][:, 0:P], ident[:])
-        nc.scalar.copy(out=gt[:], in_=bank[:])
+            nc.tensor.transpose(gbank[:, c, :], gexp[:, c, :], ident[:])
+        nc.scalar.copy(out=gt[:], in_=gbank[:])
+        for m in range(MC):
+            pb = tps.tile([P, 512], F32, name="pb", tag="tp")
+            nc.tensor.matmul(out=pb[:], lhsT=ones[:], rhs=bias_row[:, 512 * m : 512 * m + 512], start=True, stop=True)
+            nc.scalar.copy(out=bias_sb[:, 512 * m : 512 * m + 512], in_=pb[:])
 
-        for t in range(3):
-            rows_to_codes(b_raw[t], bq[:, t], bs[:, t])
-        ut = [accs.tile([P, 4, P], F32, name="ut%d" % nb, tag="acc") for nb in range(NB)]
+        gx0 = turn_block(p0, True, nc.scalar.copy)
+        gx1 = turn_block(p1, True, nc.scalar.copy)
+        p2 = part(b_raw[2])
+        quantise_block(gx0, bq[:, 0], bs[:, 0])
+        p3 = part(b_raw[3])
+        quantise_block(gx1, bq[:, 1], bs[:, 1])
+        gx2 = turn_block(p2, True, nc.scalar.copy)
+        ut = []
         for nb in range(NB):
-            ut_passes(ut, 0, nb)
-        rows_to_codes(b_raw[3], bq[:, 3], bs[:, 3])
-        for nb in range(NB):
-            ut_passes(ut, 1, nb)
-        wg = w_tile()
-        w_half(0, 0, wg)
-        for nb in range(NB):
-            ut_passes(ut, 2, nb)
-        w_half(0, 1, wg)
-        z1 = a_sort(0)
-        for nb in range(NB):
-            ut_passes(ut, 3, nb)
-        y = a_transposes(0, z1)
+            u_acc = accs.tile([P, 4, P], F32, name="ut%d" % nb, tag="acc")
+            ut.append(u_acc)
+        ut_passes(0)
+        h0 = part_half(0)
+        quantise_block(gx2, bq[:, 2], bs[:, 2])
+        gx3 = turn_block(p3, True, nc.scalar.copy)
+        ut_passes(1)
+        wg0 = turn_half(h0)
+        h1 = part_half(1)
+        quantise_block(gx3, bq[:, 3], bs[:, 3])
+        ut_passes(2)
+        quantise_half(0, wg0)
+        wg1 = turn_half(h1)
+        ut_passes(3)
         h_block(0)
-        w_quantise(0, wg)
-        for nb in range(1, NB):
-            h_block(nb)
-        a_quantise(0, y)
+        h_block(1)
+        quantise_half(1, wg1)
+        h_block(2)
+        h_block(3)
+        z1 = sort_a(0)
         nc.vector.quantize_mx(
             out=hq[:].rearrange("p c n -> p (c n)").bitcast(FP8X4),
             scales=hs[:].rearrange("p c n -> p (c n)"),
             in_=hg[:].rearrange("p c n t -> p (c n t)"),
         )
 
-        late = []
-        for m in range(MC - 1):
-            wg = w_tile()
-            w_half(m + 1, 0, wg)
-            for nb, acc in late:
-                finish(m - 1, nb, acc)
-            accl = [base(m, 0), base(m, 1)]
-            w_half(m + 1, 1, wg)
-            accl.append(base(m, 2))
-            accl.append(base(m, 3))
-            if m == 1:
-                z1 = a_sort(1)
-                y = a_transposes(1, z1)
-            for nb in range(NB):
-                delta(m, nb, accl[nb])
-            w_quantise(m + 1, wg)
-            if m == 1:
-                a_quantise(1, y)
-            finish(m, 0, accl[0])
-            finish(m, 1, accl[1])
-            late = [(2, accl[2]), (3, accl[3])]
+        base(0, 0)
+        base(0, 1)
+        h2 = part_half(2)
+        y = turn_a(z1)
+        base(0, 2)
+        wg2 = turn_half(h2)
+        quantise_a(0, y)
+        h3 = part_half(3)
+        base(0, 3)
+        delta(0, 0)
+        quantise_half(2, wg2)
+        wg3 = turn_half(h3)
+        delta(0, 1)
+        delta(0, 2)
+        delta(0, 3)
+        finish(0, 0)
+        finish(0, 1)
+        h4 = part_half(4)
+        quantise_half(3, wg3)
+        finish(0, 2)
+        finish(0, 3)
 
-        for nb, acc in late:
-            finish(MC - 2, nb, acc)
+        z1 = sort_a(1)
+        wg4 = turn_half(h4)
+        group(1, 0)
+        group(1, 1)
+        quantise_half(4, wg4)
+        h5 = part_half(5)
+        y = turn_a(z1)
+        finish(1, 0)
+        group(1, 2)
+        finish(1, 1)
+        wg5 = turn_half(h5)
+        quantise_a(1, y)
+        h6 = part_half(6)
+        group(1, 3)
+        finish(1, 2)
+        quantise_half(5, wg5)
+        finish(1, 3)
+
+        wg6 = turn_half(h6)
+        h7 = part_half(7)
+        group(2, 0)
+        group(2, 1)
+        quantise_half(6, wg6)
+        finish(2, 0)
+        wg7 = turn_half(h7)
+        finish(2, 1)
+        group(2, 2)
+        group(2, 3)
+        quantise_half(7, wg7)
+        finish(2, 2)
+        finish(2, 3)
         for nb in range(NB):
-            acc = base(MC - 1, nb)
-            delta(MC - 1, nb, acc)
-            finish(MC - 1, nb, acc)
+            group(3, nb)
+            finish(3, nb)

@@ -23,6 +23,7 @@ NB = N_TOK // P
 G = D_IN // 512
 MC = D_OUT // 512
 GATE_THRESHOLD = 0.05
+HEAD = 6
 
 FLOPS = 2 * N_TOK * D_IN * D_OUT + 2 * N_TOK * D_IN * KR + 2 * N_TOK * KR * D_OUT
 
@@ -38,7 +39,7 @@ def tile_submatrixlinear_pa_kernel(tc, x, scores, Wb, bb, A, B, out):
         accs = ctx.enter_context(tc.psum_pool(name="accs", bufs=4))
         ctx.enter_context(tc.manual_schedule())
 
-        bias_sb = const.tile([P, D_OUT], F32, name="bias_sb")
+        bias_sb = const.tile([P, D_OUT], BF16, name="bias_sb")
         gt = const.tile([P, NB, P], F32, name="gt")
         xq = const.tile([P, NB, G, P], U32, name="xq", align_bytes=64)
         xs = const.tile([P, NB, G, P], U8, name="xs", align_bytes=64)
@@ -58,7 +59,12 @@ def tile_submatrixlinear_pa_kernel(tc, x, scores, Wb, bb, A, B, out):
 
         sc_b = const.tile([P, NB, N_EXP], BF16, name="sc_b")
         nc.scalar.dma_start(out=sc_b[:], in_=scores.rearrange("(p c) k -> p c k", c=NB))
+        ones = const.tile([P, P], BF16, name="ones")
+        nc.vector.memset(ones[:], 1.0)
+        zeros = const.tile([P, 512], BF16, name="zeros")
+        nc.vector.memset(zeros[:], 0.0)
         bias_row = const.tile([P, D_OUT], BF16, name="bias_row")
+        nc.vector.memset(bias_row[:], 0.0)
 
         def load_rows(src, cuts=1):
             t = raw.tile([P, D_IN], BF16, name="rows", tag="raw")
@@ -74,64 +80,63 @@ def tile_submatrixlinear_pa_kernel(tc, x, scores, Wb, bb, A, B, out):
             )
             return z
 
-        nc.gpsimd.memset(bias_row[:].bitcast(F32), 0.0)
         ident = const.tile([P, P], F32, name="ident")
         make_identity(nc, ident[:])
-        ones = const.tile([P, P], BF16, name="ones")
-        nc.vector.memset(ones[:], 1.0)
 
-        x_raw = [load_rows(xv[c], 2 if c == 0 else 1) for c in range(NB)]
-        nc.sync.dma_start(out=bias_row[0:1, :], in_=bb.rearrange("(o n) -> o n", o=1))
+        x_raw = []
+        for c in range(NB):
+            x_raw.append(load_rows(xv[c], 2 if c == 0 else 1))
+            if c == 1:
+                nc.sync.dma_start(out=bias_row[0:1, :], in_=bb.rearrange("(o n) -> o n", o=1))
         b_raw = [load_rows(Bv[t]) for t in range(4)]
         w_raw = []
         z0 = []
-        for m in range(MC):
-            for j in range(4):
-                w_raw.append(load_rows(Wb[512 * m + P * j : 512 * m + P * j + P, :]))
-            if m < 2:
-                z0.append(load_a(m))
+        for i in range(D_OUT // P):
+            w_raw.append(load_rows(Wb[P * i : P * i + P, :]))
+            if i in (5, 9):
+                z0.append(load_a(len(z0)))
 
         mx = const.tile([P, NB], F32, name="mx")
-        nc.vector.tensor_reduce(out=mx[:], in_=sc_b[:], axis=AX.X, op=ALU.max)
         dif = const.tile([P, NB, N_EXP], F32, name="dif")
-        nc.vector.tensor_tensor(
-            out=dif[:], in0=sc_b[:], in1=mx[:].unsqueeze(2).to_broadcast([P, NB, N_EXP]), op=ALU.subtract
-        )
         ex = const.tile([P, NB, N_EXP], F32, name="ex")
-        nc.scalar.activation(out=ex[:], in_=dif[:], func=ACT.Exp)
         sm = const.tile([P, NB], F32, name="sm")
-        nc.vector.tensor_reduce(out=sm[:], in_=ex[:], axis=AX.X, op=ALU.add)
-        rs = const.tile([P, NB], F32, name="rs")
-        nc.vector.reciprocal(out=rs[:], in_=sm[:])
-        g0 = const.tile([P, NB, N_EXP], F32, name="g0")
-        nc.vector.tensor_tensor(
-            out=g0[:], in0=ex[:], in1=rs[:].unsqueeze(2).to_broadcast([P, NB, N_EXP]), op=ALU.mult
-        )
+        keep = const.tile([P, NB, N_EXP], F32, name="keep")
         g1 = const.tile([P, NB, N_EXP], F32, name="g1")
-        nc.vector.scalar_tensor_tensor(
-            out=g1[:].rearrange("p c k -> p (c k)"),
-            in0=g0[:].rearrange("p c k -> p (c k)"),
-            scalar=GATE_THRESHOLD,
-            in1=g0[:].rearrange("p c k -> p (c k)"),
-            op0=ALU.is_gt,
-            op1=ALU.mult,
-        )
         s1 = const.tile([P, NB], F32, name="s1")
-        nc.vector.tensor_reduce(out=s1[:], in_=g1[:], axis=AX.X, op=ALU.add)
-        s1m = const.tile([P, NB], F32, name="s1m")
-        nc.vector.tensor_scalar_max(out=s1m[:], in0=s1[:], scalar1=1e-8)
         r1 = const.tile([P, NB], F32, name="r1")
-        nc.vector.reciprocal(out=r1[:], in_=s1m[:])
         gexp = const.tile([P, NB, P], F32, name="gexp")
-        for nb in range(NB):
-            nc.gpsimd.tensor_scalar(
-                out=gexp[:, nb, :].rearrange("p (k j) -> p k j", j=8),
-                in0=g1[:, nb, :].unsqueeze(2).to_broadcast([P, N_EXP, 8]),
-                scalar1=r1[:, nb : nb + 1],
-                scalar2=0.0,
-                op0=ALU.mult,
-                op1=ALU.add,
+
+        def gates_a():
+            nc.vector.tensor_reduce(out=mx[:], in_=sc_b[:], axis=AX.X, op=ALU.max)
+            nc.gpsimd.tensor_tensor(
+                out=dif[:], in0=sc_b[:], in1=mx[:].unsqueeze(2).to_broadcast([P, NB, N_EXP]), op=ALU.subtract
             )
+            nc.scalar.activation(out=ex[:], in_=dif[:], func=ACT.Exp)
+
+        def gates_b():
+            nc.vector.tensor_reduce(out=sm[:], in_=ex[:], axis=AX.X, op=ALU.add)
+            nc.vector.scalar_tensor_tensor(
+                out=keep[:],
+                in0=sm[:].unsqueeze(2).to_broadcast([P, NB, N_EXP]),
+                scalar=GATE_THRESHOLD,
+                in1=ex[:],
+                op0=ALU.mult,
+                op1=ALU.is_lt,
+            )
+            nc.gpsimd.tensor_tensor(out=g1[:], in0=ex[:], in1=keep[:], op=ALU.mult)
+
+        def gates_c():
+            nc.vector.tensor_reduce(out=s1[:], in_=g1[:], axis=AX.X, op=ALU.add)
+            nc.vector.reciprocal(out=r1[:], in_=s1[:])
+            for nb in range(NB):
+                nc.gpsimd.tensor_scalar(
+                    out=gexp[:, nb, :].rearrange("p (k j) -> p k j", j=8),
+                    in0=g1[:, nb, :].unsqueeze(2).to_broadcast([P, N_EXP, 8]),
+                    scalar1=r1[:, nb : nb + 1],
+                    scalar2=0.0,
+                    op0=ALU.mult,
+                    op1=ALU.add,
+                )
 
         def psum_bank():
             bank = tps.tile([P, 4, P], F32, name="bank", tag="tp")
@@ -145,7 +150,7 @@ def tile_submatrixlinear_pa_kernel(tc, x, scores, Wb, bb, A, B, out):
             )
             return t
 
-        def turn_block(src, parted, second):
+        def turn_block(src, parted):
             gx = work.tile([P, D_IN], BF16, name="gx", tag="gx", align_bytes=64)
             dst = gx[:].bitcast(F32).rearrange("p (g n u) -> p g n u", g=G, u=2)
             words = src[:].bitcast(F32)
@@ -156,8 +161,7 @@ def tile_submatrixlinear_pa_kernel(tc, x, scores, Wb, bb, A, B, out):
                         c0 = 256 * (2 * gp + g2)
                         cols = slice(c0 + P * u, c0 + P * u + P) if parted else slice(c0 + u, c0 + 256, 2)
                         nc.tensor.transpose(bank[:, 2 * g2 + u, :], words[:, cols], ident[:])
-                copy = nc.scalar.copy if gp == 0 else second
-                copy(out=dst[:, 2 * gp : 2 * gp + 2], in_=bank[:].rearrange("p (g u) n -> p g n u", u=2))
+                nc.scalar.copy(out=dst[:, 2 * gp : 2 * gp + 2], in_=bank[:].rearrange("p (g u) n -> p g n u", u=2))
             return gx
 
         def quantise_block(gx, codes, scales):
@@ -280,51 +284,71 @@ def tile_submatrixlinear_pa_kernel(tc, x, scores, Wb, bb, A, B, out):
             )
             nc.sync.dma_start(out=outv[nb][:, 512 * m : 512 * m + 512], in_=o[:])
 
-        gx0 = turn_block(x_raw[0], False, nc.vector.tensor_copy)
-        gx1 = turn_block(x_raw[1], False, nc.vector.tensor_copy)
+        def dummies(n):
+            for i in range(n):
+                pd = tps.tile([P, 512], F32, name="pd", tag="tp")
+                nc.tensor.matmul(out=pd[:], lhsT=ones[:], rhs=zeros[:], start=True, stop=True)
+
+        def bias_cols(i):
+            pb = tps.tile([P, 1024], BF16, name="pb", tag="tp")
+            for j in range(2):
+                c0 = 1024 * i + 512 * j
+                nc.tensor.matmul(
+                    out=pb[:, 512 * j : 512 * j + 512], lhsT=ones[:], rhs=bias_row[:, c0 : c0 + 512], start=True, stop=True
+                )
+            nc.scalar.copy(out=bias_sb[:, 1024 * i : 1024 * i + 1024], in_=pb[:])
+
+        def xblk(c):
+            return turn_block(x_raw[c], False)
+
+        dummies(HEAD)
+        gates_a()
+        gx0 = xblk(0)
+        gates_b()
+        gx1 = xblk(1)
         quantise_block(gx0, xq[:, 0], xs[:, 0])
-        gx2 = turn_block(x_raw[2], False, nc.vector.tensor_copy)
+        gx2 = xblk(2)
+        gates_c()
         quantise_block(gx1, xq[:, 1], xs[:, 1])
-        gx3 = turn_block(x_raw[3], False, nc.vector.tensor_copy)
+        bias_cols(0)
+        gx3 = xblk(3)
         quantise_block(gx2, xq[:, 2], xs[:, 2])
+        bias_cols(1)
         p0 = part(b_raw[0])
         quantise_block(gx3, xq[:, 3], xs[:, 3])
         p1 = part(b_raw[1])
 
+        gb0 = turn_block(p0, True)
         gbank = psum_bank()
         for c in range(NB):
             nc.tensor.transpose(gbank[:, c, :], gexp[:, c, :], ident[:])
+        gb1 = turn_block(p1, True)
         nc.scalar.copy(out=gt[:], in_=gbank[:])
-        for m in range(MC):
-            pb = tps.tile([P, 512], F32, name="pb", tag="tp")
-            nc.tensor.matmul(out=pb[:], lhsT=ones[:], rhs=bias_row[:, 512 * m : 512 * m + 512], start=True, stop=True)
-            nc.scalar.copy(out=bias_sb[:, 512 * m : 512 * m + 512], in_=pb[:])
-
-        gx0 = turn_block(p0, True, nc.scalar.copy)
-        gx1 = turn_block(p1, True, nc.scalar.copy)
         p2 = part(b_raw[2])
-        quantise_block(gx0, bq[:, 0], bs[:, 0])
-        p3 = part(b_raw[3])
-        quantise_block(gx1, bq[:, 1], bs[:, 1])
-        gx2 = turn_block(p2, True, nc.scalar.copy)
+        quantise_block(gb0, bq[:, 0], bs[:, 0])
         ut = []
         for nb in range(NB):
             u_acc = accs.tile([P, 4, P], F32, name="ut%d" % nb, tag="acc")
             ut.append(u_acc)
         ut_passes(0)
-        h0 = part_half(0)
-        quantise_block(gx2, bq[:, 2], bs[:, 2])
-        gx3 = turn_block(p3, True, nc.scalar.copy)
+        gb2 = turn_block(p2, True)
+        p3 = part(b_raw[3])
+        quantise_block(gb1, bq[:, 1], bs[:, 1])
         ut_passes(1)
-        wg0 = turn_half(h0)
-        h1 = part_half(1)
-        quantise_block(gx3, bq[:, 3], bs[:, 3])
+        gb3 = turn_block(p3, True)
+        h0 = part_half(0)
+        quantise_block(gb2, bq[:, 2], bs[:, 2])
         ut_passes(2)
+        wg0 = turn_half(h0)
+        quantise_block(gb3, bq[:, 3], bs[:, 3])
+        h1 = part_half(1)
+        ut_passes(3)
         quantise_half(0, wg0)
         wg1 = turn_half(h1)
-        ut_passes(3)
+        h2 = part_half(2)
         h_block(0)
         h_block(1)
+        wg2 = turn_half(h2)
         quantise_half(1, wg1)
         h_block(2)
         h_block(3)
@@ -337,34 +361,30 @@ def tile_submatrixlinear_pa_kernel(tc, x, scores, Wb, bb, A, B, out):
 
         base(0, 0)
         base(0, 1)
-        h2 = part_half(2)
+        quantise_half(2, wg2)
+        h3 = part_half(3)
         y = turn_a(z1)
         base(0, 2)
-        wg2 = turn_half(h2)
-        quantise_a(0, y)
-        h3 = part_half(3)
         base(0, 3)
-        delta(0, 0)
-        quantise_half(2, wg2)
         wg3 = turn_half(h3)
-        delta(0, 1)
-        delta(0, 2)
-        delta(0, 3)
+        quantise_a(0, y)
+        h4 = part_half(4)
+        for nb in range(NB):
+            delta(0, nb)
         finish(0, 0)
         finish(0, 1)
-        h4 = part_half(4)
         quantise_half(3, wg3)
         finish(0, 2)
         finish(0, 3)
 
-        z1 = sort_a(1)
         wg4 = turn_half(h4)
+        z1 = sort_a(1)
         group(1, 0)
         group(1, 1)
-        quantise_half(4, wg4)
         h5 = part_half(5)
-        y = turn_a(z1)
+        quantise_half(4, wg4)
         finish(1, 0)
+        y = turn_a(z1)
         group(1, 2)
         finish(1, 1)
         wg5 = turn_half(h5)

@@ -23,7 +23,6 @@ NB = N_TOK // P
 G = D_IN // 512
 MC = D_OUT // 512
 GATE_THRESHOLD = 0.05
-HEAD = 6
 
 FLOPS = 2 * N_TOK * D_IN * D_OUT + 2 * N_TOK * D_IN * KR + 2 * N_TOK * KR * D_OUT
 
@@ -286,7 +285,7 @@ def tile_submatrixlinear_pa_kernel(tc, x, scores, Wb, bb, A, B, out):
 
         def dummies(n):
             for i in range(n):
-                pd = tps.tile([P, 512], F32, name="pd", tag="tp")
+                pd = accs.tile([P, 512], F32, name="pd", tag="acc")
                 nc.tensor.matmul(out=pd[:], lhsT=ones[:], rhs=zeros[:], start=True, stop=True)
 
         def bias_cols(i):
@@ -301,12 +300,14 @@ def tile_submatrixlinear_pa_kernel(tc, x, scores, Wb, bb, A, B, out):
         def xblk(c):
             return turn_block(x_raw[c], False)
 
-        dummies(HEAD)
+        dummies(4)
         gates_a()
         gx0 = xblk(0)
+        dummies(2)
         gates_b()
         gx1 = xblk(1)
         quantise_block(gx0, xq[:, 0], xs[:, 0])
+        dummies(2)
         gx2 = xblk(2)
         gates_c()
         quantise_block(gx1, xq[:, 1], xs[:, 1])
@@ -322,6 +323,7 @@ def tile_submatrixlinear_pa_kernel(tc, x, scores, Wb, bb, A, B, out):
         gbank = psum_bank()
         for c in range(NB):
             nc.tensor.transpose(gbank[:, c, :], gexp[:, c, :], ident[:])
+        dummies(2)
         gb1 = turn_block(p1, True)
         nc.scalar.copy(out=gt[:], in_=gbank[:])
         p2 = part(b_raw[2])

@@ -62,8 +62,6 @@ def tile_submatrixlinear_pa_kernel(tc, x, scores, Wb, bb, A, B, out):
         nc.vector.memset(ones[:], 1.0)
         zeros = const.tile([P, 512], BF16, name="zeros")
         nc.vector.memset(zeros[:], 0.0)
-        bias_row = const.tile([P, D_OUT], BF16, name="bias_row")
-        nc.vector.memset(bias_row[:], 0.0)
 
         def load_rows(src, cuts=1):
             t = raw.tile([P, D_IN], BF16, name="rows", tag="raw")
@@ -83,17 +81,18 @@ def tile_submatrixlinear_pa_kernel(tc, x, scores, Wb, bb, A, B, out):
         make_identity(nc, ident[:])
 
         x_raw = []
+        b_raw = []
         for c in range(NB):
             x_raw.append(load_rows(xv[c], 2 if c == 0 else 1))
-            if c == 1:
-                nc.sync.dma_start(out=bias_row[0:1, :], in_=bb.rearrange("(o n) -> o n", o=1))
-        b_raw = [load_rows(Bv[t]) for t in range(4)]
+            b_raw.append(load_rows(Bv[c]))
         w_raw = []
         z0 = []
         for i in range(D_OUT // P):
             w_raw.append(load_rows(Wb[P * i : P * i + P, :]))
             if i in (5, 9):
                 z0.append(load_a(len(z0)))
+            if i == 7:
+                nc.sync.dma_start(out=bias_sb[:], in_=bb.partition_broadcast(P))
 
         mx = const.tile([P, NB], F32, name="mx")
         dif = const.tile([P, NB, N_EXP], F32, name="dif")
@@ -137,6 +136,9 @@ def tile_submatrixlinear_pa_kernel(tc, x, scores, Wb, bb, A, B, out):
                     op1=ALU.add,
                 )
 
+        x_turned, b_parted, b_turned, w_parted, w_turned = {}, {}, {}, {}, {}
+        a_sorted, a_turned, ut, acc = {}, {}, {}, {}
+
         def psum_bank():
             bank = tps.tile([P, 4, P], F32, name="bank", tag="tp")
             return bank
@@ -170,18 +172,19 @@ def tile_submatrixlinear_pa_kernel(tc, x, scores, Wb, bb, A, B, out):
                 in_=gx[:],
             )
 
-        def ut_passes(t):
-            for nb in range(NB):
-                for g in range(G):
-                    nc.tensor.matmul_mx(
-                        out=ut[nb][:, t, :],
-                        lhsT=bq[:, t, g, :].bitcast(FP8X4),
-                        lhsT_scale=bs[:, t, g, :],
-                        rhs=xq[:, nb, g, :].bitcast(FP8X4),
-                        rhs_scale=xs[:, nb, g, :],
-                        start=(g == 0),
-                        stop=(g == G - 1),
-                    )
+        def u_passes(t, nb):
+            if nb not in ut:
+                ut[nb] = accs.tile([P, 4, P], F32, name="ut%d" % nb, tag="acc")
+            for g in range(G):
+                nc.tensor.matmul_mx(
+                    out=ut[nb][:, t, :],
+                    lhsT=bq[:, t, g, :].bitcast(FP8X4),
+                    lhsT_scale=bs[:, t, g, :],
+                    rhs=xq[:, nb, g, :].bitcast(FP8X4),
+                    rhs_scale=xs[:, nb, g, :],
+                    start=(g == 0),
+                    stop=(g == G - 1),
+                )
 
         def h_block(nb):
             nc.vector.tensor_tensor(
@@ -191,29 +194,27 @@ def tile_submatrixlinear_pa_kernel(tc, x, scores, Wb, bb, A, B, out):
                 op=ALU.mult,
             )
 
-        def turn_half(pair):
+        def turn_w(s):
             wg = work.tile([P, 2 * D_IN], BF16, name="wg", tag="wg", align_bytes=64)
             dst = wg[:].bitcast(F32).rearrange("p (g j n u) -> p g j n u", g=G, j=2, u=2)
             for g in range(G):
                 bank = psum_bank()
                 for j in range(2):
                     for u in range(2):
-                        c0 = 256 * g + P * u
-                        nc.tensor.transpose(bank[:, 2 * j + u, :], pair[j][:].bitcast(F32)[:, c0 : c0 + P], ident[:])
+                        c0 = 256 * g
+                        cols = slice(c0 + P * u, c0 + P * u + P)
+                        nc.tensor.transpose(bank[:, 2 * j + u, :], w_parted[2 * s + j][:].bitcast(F32)[:, cols], ident[:])
                 nc.scalar.copy(out=dst[:, g], in_=bank[:].rearrange("p (j u) n -> p j n u", u=2))
-            return wg
+            w_turned[s] = wg
 
-        def quantise_half(s, wg):
+        def quantise_w(s):
             m, c0 = s // 2, 256 * (s % 2)
             for g in range(G):
                 nc.vector.quantize_mx(
                     out=wq[:, m, g, c0 : c0 + 256].bitcast(FP8X4),
                     scales=ws[:, m, g, c0 : c0 + 256],
-                    in_=wg[:, 1024 * g : 1024 * g + 1024],
+                    in_=w_turned[s][:, 1024 * g : 1024 * g + 1024],
                 )
-
-        def part_half(s):
-            return [part(w_raw[2 * s]), part(w_raw[2 * s + 1])]
 
         def sort_a(half):
             z1 = work.tile([P, 4096], BF16, name="z1", tag="z1", bufs=1)
@@ -222,30 +223,29 @@ def tile_submatrixlinear_pa_kernel(tc, x, scores, Wb, bb, A, B, out):
             zi = zi.rearrange("p (k b j u) -> p u b k j", k=N_EXP, b=8, u=2)
             nc.scalar.copy(out=zo[:, 0], in_=zi[:, 0])
             nc.vector.tensor_copy(out=zo[:, 1], in_=zi[:, 1])
-            return z1
+            a_sorted[half] = z1
 
-        def turn_a(z1):
+        def turn_a(half):
             y = work.tile([P, 4096], BF16, name="y", tag="y", bufs=1, align_bytes=64)
             yw = y[:].bitcast(F32).rearrange("p (w h bu) -> p h w bu", w=P, h=4)
-            zw = z1[:].bitcast(F32)
+            zw = a_sorted[half][:].bitcast(F32)
             for h in range(4):
                 bank = psum_bank()
                 for i in range(4):
                     c0 = P * (4 * h + i)
                     nc.tensor.transpose(bank[:, i, :], zw[:, c0 : c0 + P], ident[:])
                 nc.scalar.copy(out=yw[:, h], in_=bank[:].rearrange("p bu w -> p w bu"))
-            return y
+            a_turned[half] = y
 
-        def quantise_a(half, y):
+        def quantise_a(half):
             for i in range(2):
                 c0 = 1024 * half + 512 * i
                 nc.vector.quantize_mx(
                     out=aq[:, c0 : c0 + 512].bitcast(FP8X4),
                     scales=asc[:, c0 : c0 + 512],
-                    in_=y[:, 2048 * i : 2048 * i + 2048],
+                    in_=a_turned[half][:, 2048 * i : 2048 * i + 2048],
                 )
 
-        acc = {}
 
         def base(m, nb):
             t = accs.tile([P, 512], F32, name="acc", tag="acc")
@@ -272,10 +272,6 @@ def tile_submatrixlinear_pa_kernel(tc, x, scores, Wb, bb, A, B, out):
                 stop=True,
             )
 
-        def group(m, nb):
-            base(m, nb)
-            delta(m, nb)
-
         def finish(m, nb):
             o = outp.tile([P, 512], F32, name="o", tag="o")
             nc.vector.tensor_tensor(
@@ -288,128 +284,166 @@ def tile_submatrixlinear_pa_kernel(tc, x, scores, Wb, bb, A, B, out):
                 pd = accs.tile([P, 512], F32, name="pd", tag="acc")
                 nc.tensor.matmul(out=pd[:], lhsT=ones[:], rhs=zeros[:], start=True, stop=True)
 
-        def bias_cols(i):
-            pb = tps.tile([P, 1024], BF16, name="pb", tag="tp")
-            for j in range(2):
-                c0 = 1024 * i + 512 * j
-                nc.tensor.matmul(
-                    out=pb[:, 512 * j : 512 * j + 512], lhsT=ones[:], rhs=bias_row[:, c0 : c0 + 512], start=True, stop=True
-                )
-            nc.scalar.copy(out=bias_sb[:, 1024 * i : 1024 * i + 1024], in_=pb[:])
+        def turn_x(c):
+            x_turned[c] = turn_block(x_raw[c], False)
 
-        def xblk(c):
-            return turn_block(x_raw[c], False)
+        def quantise_x(c):
+            quantise_block(x_turned[c], xq[:, c], xs[:, c])
+
+        def part_b(t):
+            b_parted[t] = part(b_raw[t])
+
+        def turn_b(t):
+            b_turned[t] = turn_block(b_parted[t], True) if t in b_parted else turn_block(b_raw[t], False)
+
+        def quantise_b(t):
+            quantise_block(b_turned[t], bq[:, t], bs[:, t])
+
+        def part_w(i):
+            w_parted[i] = part(w_raw[i])
+
+        def turn_gates():
+            bank = psum_bank()
+            for c in range(NB):
+                nc.tensor.transpose(bank[:, c, :], gexp[:, c, :], ident[:])
+            nc.scalar.copy(out=gt[:], in_=bank[:])
+
+        def quantise_h():
+            nc.vector.quantize_mx(
+                out=hq[:].rearrange("p c n -> p (c n)").bitcast(FP8X4),
+                scales=hs[:].rearrange("p c n -> p (c n)"),
+                in_=hg[:].rearrange("p c n t -> p (c n t)"),
+            )
 
         dummies(4)
         gates_a()
-        gx0 = xblk(0)
+        turn_x(0)
         dummies(2)
         gates_b()
-        gx1 = xblk(1)
-        quantise_block(gx0, xq[:, 0], xs[:, 0])
+        turn_b(0)
+        quantise_x(0)
+        turn_x(1)
+        quantise_b(0)
         dummies(2)
-        gx2 = xblk(2)
+        turn_b(1)
         gates_c()
-        quantise_block(gx1, xq[:, 1], xs[:, 1])
-        bias_cols(0)
-        gx3 = xblk(3)
-        quantise_block(gx2, xq[:, 2], xs[:, 2])
-        bias_cols(1)
-        p0 = part(b_raw[0])
-        quantise_block(gx3, xq[:, 3], xs[:, 3])
-        p1 = part(b_raw[1])
-
-        gb0 = turn_block(p0, True)
-        gbank = psum_bank()
-        for c in range(NB):
-            nc.tensor.transpose(gbank[:, c, :], gexp[:, c, :], ident[:])
-        dummies(2)
-        gb1 = turn_block(p1, True)
-        nc.scalar.copy(out=gt[:], in_=gbank[:])
-        p2 = part(b_raw[2])
-        quantise_block(gb0, bq[:, 0], bs[:, 0])
-        ut = []
-        for nb in range(NB):
-            u_acc = accs.tile([P, 4, P], F32, name="ut%d" % nb, tag="acc")
-            ut.append(u_acc)
-        ut_passes(0)
-        gb2 = turn_block(p2, True)
-        p3 = part(b_raw[3])
-        quantise_block(gb1, bq[:, 1], bs[:, 1])
-        ut_passes(1)
-        gb3 = turn_block(p3, True)
-        h0 = part_half(0)
-        quantise_block(gb2, bq[:, 2], bs[:, 2])
-        ut_passes(2)
-        wg0 = turn_half(h0)
-        quantise_block(gb3, bq[:, 3], bs[:, 3])
-        h1 = part_half(1)
-        ut_passes(3)
-        quantise_half(0, wg0)
-        wg1 = turn_half(h1)
-        h2 = part_half(2)
+        quantise_x(1)
+        turn_x(2)
+        part_b(2)
+        quantise_b(1)
+        u_passes(0, 0)
+        u_passes(0, 1)
+        u_passes(1, 0)
+        turn_b(2)
+        quantise_x(2)
+        part_b(3)
+        turn_x(3)
+        u_passes(1, 1)
+        quantise_b(2)
+        turn_b(3)
+        turn_gates()
+        quantise_x(3)
+        u_passes(0, 2)
+        u_passes(1, 2)
+        u_passes(2, 0)
+        u_passes(2, 1)
+        u_passes(2, 2)
+        part_w(0)
+        part_w(1)
+        turn_w(0)
+        quantise_b(3)
+        part_w(2)
+        part_w(3)
+        u_passes(0, 3)
+        u_passes(3, 0)
+        u_passes(3, 1)
+        u_passes(3, 2)
+        quantise_w(0)
+        turn_w(1)
+        part_w(4)
+        part_w(5)
+        u_passes(1, 3)
+        u_passes(2, 3)
+        u_passes(3, 3)
         h_block(0)
         h_block(1)
-        wg2 = turn_half(h2)
-        quantise_half(1, wg1)
+        quantise_w(1)
         h_block(2)
         h_block(3)
-        z1 = sort_a(0)
-        nc.vector.quantize_mx(
-            out=hq[:].rearrange("p c n -> p (c n)").bitcast(FP8X4),
-            scales=hs[:].rearrange("p c n -> p (c n)"),
-            in_=hg[:].rearrange("p c n t -> p (c n t)"),
-        )
-
+        quantise_h()
+        turn_w(2)
+        sort_a(0)
+        part_w(6)
+        part_w(7)
         base(0, 0)
         base(0, 1)
-        quantise_half(2, wg2)
-        h3 = part_half(3)
-        y = turn_a(z1)
+        quantise_w(2)
+        turn_a(0)
         base(0, 2)
-        base(0, 3)
-        wg3 = turn_half(h3)
-        quantise_a(0, y)
-        h4 = part_half(4)
-        for nb in range(NB):
-            delta(0, nb)
+        part_w(8)
+        part_w(9)
+        turn_w(3)
+        quantise_a(0)
+        delta(0, 0)
+        delta(0, 1)
+        delta(0, 2)
+        sort_a(1)
+        quantise_w(3)
         finish(0, 0)
         finish(0, 1)
-        quantise_half(3, wg3)
+        base(0, 3)
+        delta(0, 3)
+        turn_w(4)
+        part_w(10)
+        part_w(11)
         finish(0, 2)
+        quantise_w(4)
         finish(0, 3)
-
-        wg4 = turn_half(h4)
-        z1 = sort_a(1)
-        group(1, 0)
-        group(1, 1)
-        h5 = part_half(5)
-        quantise_half(4, wg4)
+        base(1, 0)
+        delta(1, 0)
+        turn_a(1)
+        quantise_a(1)
+        part_w(12)
+        part_w(13)
         finish(1, 0)
-        y = turn_a(z1)
-        group(1, 2)
+        base(1, 1)
+        delta(1, 1)
+        turn_w(5)
+        quantise_w(5)
         finish(1, 1)
-        wg5 = turn_half(h5)
-        quantise_a(1, y)
-        h6 = part_half(6)
-        group(1, 3)
+        part_w(14)
+        part_w(15)
+        base(1, 2)
+        delta(1, 2)
+        turn_w(6)
+        quantise_w(6)
         finish(1, 2)
-        quantise_half(5, wg5)
+        base(1, 3)
+        delta(1, 3)
+        turn_w(7)
+        quantise_w(7)
         finish(1, 3)
-
-        wg6 = turn_half(h6)
-        h7 = part_half(7)
-        group(2, 0)
-        group(2, 1)
-        quantise_half(6, wg6)
+        base(2, 0)
+        delta(2, 0)
         finish(2, 0)
-        wg7 = turn_half(h7)
+        base(2, 1)
+        delta(2, 1)
         finish(2, 1)
-        group(2, 2)
-        group(2, 3)
-        quantise_half(7, wg7)
+        base(2, 2)
+        delta(2, 2)
         finish(2, 2)
+        base(2, 3)
+        delta(2, 3)
         finish(2, 3)
-        for nb in range(NB):
-            group(3, nb)
-            finish(3, nb)
+        base(3, 0)
+        delta(3, 0)
+        finish(3, 0)
+        base(3, 1)
+        delta(3, 1)
+        finish(3, 1)
+        base(3, 2)
+        delta(3, 2)
+        finish(3, 2)
+        base(3, 3)
+        delta(3, 3)
+        finish(3, 3)

@@ -62,6 +62,8 @@ def tile_submatrixlinear_pa_kernel(tc, x, scores, Wb, bb, A, B, out):
         nc.vector.memset(ones[:], 1.0)
         zeros = const.tile([P, 512], BF16, name="zeros")
         nc.vector.memset(zeros[:], 0.0)
+        bias_row = const.tile([P, D_OUT], BF16, name="bias_row")
+        nc.vector.memset(bias_row[:], 0.0)
 
         def load_rows(src, cuts=1):
             t = raw.tile([P, D_IN], BF16, name="rows", tag="raw")
@@ -85,14 +87,14 @@ def tile_submatrixlinear_pa_kernel(tc, x, scores, Wb, bb, A, B, out):
         for c in range(NB):
             x_raw.append(load_rows(xv[c], 2 if c == 0 else 1))
             b_raw.append(load_rows(Bv[c]))
+            if c == 0:
+                nc.sync.dma_start(out=bias_row[0:1, :], in_=bb.rearrange("(o n) -> o n", o=1))
         w_raw = []
         z0 = []
         for i in range(D_OUT // P):
             w_raw.append(load_rows(Wb[P * i : P * i + P, :]))
             if i in (5, 9):
                 z0.append(load_a(len(z0)))
-            if i == 7:
-                nc.sync.dma_start(out=bias_sb[:], in_=bb.partition_broadcast(P))
 
         mx = const.tile([P, NB], F32, name="mx")
         dif = const.tile([P, NB, N_EXP], F32, name="dif")
@@ -284,6 +286,15 @@ def tile_submatrixlinear_pa_kernel(tc, x, scores, Wb, bb, A, B, out):
                 pd = accs.tile([P, 512], F32, name="pd", tag="acc")
                 nc.tensor.matmul(out=pd[:], lhsT=ones[:], rhs=zeros[:], start=True, stop=True)
 
+        def bias_cols(i):
+            pb = tps.tile([P, 1024], BF16, name="pb", tag="tp")
+            for j in range(2):
+                c0 = 1024 * i + 512 * j
+                nc.tensor.matmul(
+                    out=pb[:, 512 * j : 512 * j + 512], lhsT=ones[:], rhs=bias_row[:, c0 : c0 + 512], start=True, stop=True
+                )
+            nc.scalar.copy(out=bias_sb[:, 1024 * i : 1024 * i + 1024], in_=pb[:])
+
         def turn_x(c):
             x_turned[c] = turn_block(x_raw[c], False)
 
@@ -324,11 +335,12 @@ def tile_submatrixlinear_pa_kernel(tc, x, scores, Wb, bb, A, B, out):
         quantise_x(0)
         turn_x(1)
         quantise_b(0)
-        dummies(2)
+        bias_cols(0)
         turn_b(1)
         gates_c()
         quantise_x(1)
         turn_x(2)
+        bias_cols(1)
         part_b(2)
         quantise_b(1)
         u_passes(0, 0)

@@ -281,6 +281,34 @@ def tile_submatrixlinear_pa_kernel(tc, x, scores, Wb, bb, A, B, out):
             )
             nc.sync.dma_start(out=outv[nb][:, 512 * m : 512 * m + 512], in_=o[:])
 
+        def last_group(m, nb):
+            for i in range(2):
+                t = accs.tile([P, 256], F32, name="half", tag="acc")
+                cols = slice(256 * i, 256 * i + 256)
+                for g in range(G):
+                    nc.tensor.matmul_mx(
+                        out=t[:],
+                        lhsT=xq[:, nb, g, :].bitcast(FP8X4),
+                        lhsT_scale=xs[:, nb, g, :],
+                        rhs=wq[:, m, g, cols].bitcast(FP8X4),
+                        rhs_scale=ws[:, m, g, cols],
+                        start=(g == 0),
+                        stop=False,
+                    )
+                c0 = 512 * m + 256 * i
+                nc.tensor.matmul_mx(
+                    out=t[:],
+                    lhsT=hq[:, nb, :].bitcast(FP8X4),
+                    lhsT_scale=hs[:, nb, :],
+                    rhs=aq[:, c0 : c0 + 256].bitcast(FP8X4),
+                    rhs_scale=asc[:, c0 : c0 + 256],
+                    start=False,
+                    stop=True,
+                )
+                o = outp.tile([P, 512], F32, name="o", tag="o")
+                nc.vector.tensor_tensor(out=o[:, 0:256], in0=t[:], in1=bias_sb[:, c0 : c0 + 256], op=ALU.add)
+                nc.sync.dma_start(out=outv[nb][:, c0 : c0 + 256], in_=o[:, 0:256])
+
         def dummies(n):
             for i in range(n):
                 pd = accs.tile([P, 512], F32, name="pd", tag="acc")
@@ -333,110 +361,110 @@ def tile_submatrixlinear_pa_kernel(tc, x, scores, Wb, bb, A, B, out):
         gates_b()
         turn_b(0)
         quantise_x(0)
-        turn_x(1)
-        quantise_b(0)
         bias_cols(0)
+        turn_x(1)
         turn_b(1)
         gates_c()
+        quantise_b(0)
         quantise_x(1)
+        u_passes(0, 0)
+        part_b(2)
         turn_x(2)
         bias_cols(1)
-        part_b(2)
+        turn_b(2)
         quantise_b(1)
-        u_passes(0, 0)
+        quantise_x(2)
         u_passes(0, 1)
         u_passes(1, 0)
-        turn_b(2)
-        quantise_x(2)
+        u_passes(1, 1)
         part_b(3)
         turn_x(3)
-        u_passes(1, 1)
-        quantise_b(2)
         turn_b(3)
         turn_gates()
-        quantise_x(3)
-        u_passes(0, 2)
-        u_passes(1, 2)
-        u_passes(2, 0)
-        u_passes(2, 1)
-        u_passes(2, 2)
+        quantise_b(2)
         part_w(0)
         part_w(1)
+        quantise_x(3)
+        u_passes(2, 0)
+        u_passes(2, 1)
+        u_passes(0, 2)
+        u_passes(1, 2)
+        u_passes(2, 2)
         turn_w(0)
         quantise_b(3)
         part_w(2)
         part_w(3)
-        u_passes(0, 3)
         u_passes(3, 0)
         u_passes(3, 1)
         u_passes(3, 2)
-        quantise_w(0)
-        turn_w(1)
+        u_passes(0, 3)
+        h_block(0)
         part_w(4)
+        turn_w(1)
+        quantise_w(0)
+        h_block(1)
         part_w(5)
         u_passes(1, 3)
         u_passes(2, 3)
         u_passes(3, 3)
-        h_block(0)
-        h_block(1)
-        quantise_w(1)
         h_block(2)
+        quantise_w(1)
         h_block(3)
         quantise_h()
         turn_w(2)
-        sort_a(0)
-        part_w(6)
-        part_w(7)
         base(0, 0)
         base(0, 1)
-        quantise_w(2)
-        turn_a(0)
         base(0, 2)
-        part_w(8)
-        part_w(9)
+        sort_a(0)
+        quantise_w(2)
+        part_w(6)
+        part_w(7)
+        turn_a(0)
+        base(0, 3)
         turn_w(3)
+        part_w(8)
         quantise_a(0)
+        part_w(9)
         delta(0, 0)
         delta(0, 1)
         delta(0, 2)
+        delta(0, 3)
         sort_a(1)
         quantise_w(3)
         finish(0, 0)
         finish(0, 1)
-        base(0, 3)
-        delta(0, 3)
         turn_w(4)
+        base(1, 0)
+        delta(1, 0)
         part_w(10)
         part_w(11)
         finish(0, 2)
         quantise_w(4)
         finish(0, 3)
-        base(1, 0)
-        delta(1, 0)
         turn_a(1)
-        quantise_a(1)
-        part_w(12)
-        part_w(13)
-        finish(1, 0)
         base(1, 1)
         delta(1, 1)
+        finish(1, 0)
+        part_w(12)
+        part_w(13)
+        quantise_a(1)
         turn_w(5)
-        quantise_w(5)
         finish(1, 1)
-        part_w(14)
-        part_w(15)
         base(1, 2)
         delta(1, 2)
+        part_w(14)
+        quantise_w(5)
+        part_w(15)
         turn_w(6)
-        quantise_w(6)
         finish(1, 2)
+        quantise_w(6)
         base(1, 3)
         delta(1, 3)
-        turn_w(7)
-        quantise_w(7)
-        finish(1, 3)
         base(2, 0)
         delta(2, 0)
+        turn_w(7)
+        finish(1, 3)
+        quantise_w(7)
         finish(2, 0)
         base(2, 1)
         delta(2, 1)
@@ -456,6 +484,4 @@ def tile_submatrixlinear_pa_kernel(tc, x, scores, Wb, bb, A, B, out):
         base(3, 2)
         delta(3, 2)
         finish(3, 2)
-        base(3, 3)
-        delta(3, 3)
-        finish(3, 3)
+        last_group(3, 3)

@@ -209,23 +209,24 @@ def tile_submatrixlinear_pa_kernel(tc, x, scores, Wb, bb, A, B, out):
                 nc.scalar.copy(out=dst[:, g], in_=bank[:].rearrange("p (j u) n -> p j n u", u=2))
             w_turned[s] = wg
 
-        def quantise_w(s):
+        def quantise_w(s, part_of_g):
             m, c0 = s // 2, 256 * (s % 2)
-            for g in range(G):
+            for g in part_of_g:
                 nc.vector.quantize_mx(
                     out=wq[:, m, g, c0 : c0 + 256].bitcast(FP8X4),
                     scales=ws[:, m, g, c0 : c0 + 256],
                     in_=w_turned[s][:, 1024 * g : 1024 * g + 1024],
                 )
 
-        def sort_a(half):
-            z1 = work.tile([P, 4096], BF16, name="z1", tag="z1", bufs=1)
+        def sort_a(half, u):
+            if half not in a_sorted:
+                a_sorted[half] = work.tile([P, 4096], BF16, name="z1", tag="z1", bufs=1)
+            z1 = a_sorted[half]
             zo = z1[:].bitcast(F32).rearrange("p (b u k j) -> p u b k j", b=8, u=2, k=N_EXP)
             zi = z0[half][:].rearrange("p k c -> p (k c)").bitcast(F32)
             zi = zi.rearrange("p (k b j u) -> p u b k j", k=N_EXP, b=8, u=2)
-            nc.scalar.copy(out=zo[:, 0], in_=zi[:, 0])
-            nc.vector.tensor_copy(out=zo[:, 1], in_=zi[:, 1])
-            a_sorted[half] = z1
+            copy = nc.scalar.copy if u == 0 else nc.vector.tensor_copy
+            copy(out=zo[:, u], in_=zi[:, u])
 
         def turn_a(half):
             y = work.tile([P, 4096], BF16, name="y", tag="y", bufs=1, align_bytes=64)
@@ -354,7 +355,7 @@ def tile_submatrixlinear_pa_kernel(tc, x, scores, Wb, bb, A, B, out):
                 in_=hg[:].rearrange("p c n t -> p (c n t)"),
             )
 
-        dummies(4)
+        dummies(5)
         gates_a()
         turn_x(0)
         dummies(2)
@@ -363,6 +364,7 @@ def tile_submatrixlinear_pa_kernel(tc, x, scores, Wb, bb, A, B, out):
         quantise_x(0)
         bias_cols(0)
         turn_x(1)
+        dummies(2)
         turn_b(1)
         gates_c()
         quantise_b(0)
@@ -370,7 +372,6 @@ def tile_submatrixlinear_pa_kernel(tc, x, scores, Wb, bb, A, B, out):
         u_passes(0, 0)
         part_b(2)
         turn_x(2)
-        bias_cols(1)
         turn_b(2)
         quantise_b(1)
         quantise_x(2)
@@ -379,6 +380,7 @@ def tile_submatrixlinear_pa_kernel(tc, x, scores, Wb, bb, A, B, out):
         u_passes(1, 1)
         part_b(3)
         turn_x(3)
+        bias_cols(1)
         turn_b(3)
         turn_gates()
         quantise_b(2)
@@ -401,22 +403,24 @@ def tile_submatrixlinear_pa_kernel(tc, x, scores, Wb, bb, A, B, out):
         h_block(0)
         part_w(4)
         turn_w(1)
-        quantise_w(0)
+        quantise_w(0, (0, 1))
         h_block(1)
         part_w(5)
+        quantise_w(0, (2, 3))
         u_passes(1, 3)
         u_passes(2, 3)
         u_passes(3, 3)
         h_block(2)
-        quantise_w(1)
+        quantise_w(1, (0, 1, 2, 3))
         h_block(3)
         quantise_h()
         turn_w(2)
         base(0, 0)
         base(0, 1)
         base(0, 2)
-        sort_a(0)
-        quantise_w(2)
+        sort_a(0, 0)
+        sort_a(0, 1)
+        quantise_w(2, (0, 1, 2, 3))
         part_w(6)
         part_w(7)
         turn_a(0)
@@ -428,18 +432,19 @@ def tile_submatrixlinear_pa_kernel(tc, x, scores, Wb, bb, A, B, out):
         delta(0, 0)
         delta(0, 1)
         delta(0, 2)
-        delta(0, 3)
-        sort_a(1)
-        quantise_w(3)
+        sort_a(1, 0)
+        quantise_w(3, (0, 1, 2, 3))
         finish(0, 0)
+        sort_a(1, 1)
         finish(0, 1)
         turn_w(4)
+        delta(0, 3)
         base(1, 0)
         delta(1, 0)
         part_w(10)
         part_w(11)
         finish(0, 2)
-        quantise_w(4)
+        quantise_w(4, (0, 1, 2, 3))
         finish(0, 3)
         turn_a(1)
         base(1, 1)
@@ -453,18 +458,18 @@ def tile_submatrixlinear_pa_kernel(tc, x, scores, Wb, bb, A, B, out):
         base(1, 2)
         delta(1, 2)
         part_w(14)
-        quantise_w(5)
+        quantise_w(5, (0, 1, 2, 3))
         part_w(15)
         turn_w(6)
         finish(1, 2)
-        quantise_w(6)
+        quantise_w(6, (0, 1, 2, 3))
         base(1, 3)
         delta(1, 3)
         base(2, 0)
         delta(2, 0)
         turn_w(7)
         finish(1, 3)
-        quantise_w(7)
+        quantise_w(7, (0, 1, 2, 3))
         finish(2, 0)
         base(2, 1)
         delta(2, 1)

@@ -24,6 +24,10 @@ G = D_IN // 512
 MC = D_OUT // 512
 GATE_THRESHOLD = 0.05
 
+ALL = (0, 1, 2, 3)
+LOW = (0, 1)
+HIGH = (2, 3)
+
 FLOPS = 2 * N_TOK * D_IN * D_OUT + 2 * N_TOK * D_IN * KR + 2 * N_TOK * KR * D_OUT
 
 
@@ -196,10 +200,12 @@ def tile_submatrixlinear_pa_kernel(tc, x, scores, Wb, bb, A, B, out):
                 op=ALU.mult,
             )
 
-        def turn_w(s):
-            wg = work.tile([P, 2 * D_IN], BF16, name="wg", tag="wg", align_bytes=64)
+        def turn_w(s, passes):
+            if s not in w_turned:
+                w_turned[s] = work.tile([P, 2 * D_IN], BF16, name="wg", tag="wg", align_bytes=64)
+            wg = w_turned[s]
             dst = wg[:].bitcast(F32).rearrange("p (g j n u) -> p g j n u", g=G, j=2, u=2)
-            for g in range(G):
+            for g in passes:
                 bank = psum_bank()
                 for j in range(2):
                     for u in range(2):
@@ -207,11 +213,10 @@ def tile_submatrixlinear_pa_kernel(tc, x, scores, Wb, bb, A, B, out):
                         cols = slice(c0 + P * u, c0 + P * u + P)
                         nc.tensor.transpose(bank[:, 2 * j + u, :], w_parted[2 * s + j][:].bitcast(F32)[:, cols], ident[:])
                 nc.scalar.copy(out=dst[:, g], in_=bank[:].rearrange("p (j u) n -> p j n u", u=2))
-            w_turned[s] = wg
 
-        def quantise_w(s, part_of_g):
+        def quantise_w(s, passes):
             m, c0 = s // 2, 256 * (s % 2)
-            for g in part_of_g:
+            for g in passes:
                 nc.vector.quantize_mx(
                     out=wq[:, m, g, c0 : c0 + 256].bitcast(FP8X4),
                     scales=ws[:, m, g, c0 : c0 + 256],
@@ -364,121 +369,123 @@ def tile_submatrixlinear_pa_kernel(tc, x, scores, Wb, bb, A, B, out):
         quantise_x(0)
         bias_cols(0)
         turn_x(1)
-        dummies(2)
         turn_b(1)
-        gates_c()
+        bias_cols(1)
         quantise_b(0)
+        gates_c()
         quantise_x(1)
-        u_passes(0, 0)
         part_b(2)
         turn_x(2)
-        turn_b(2)
-        quantise_b(1)
-        quantise_x(2)
+        u_passes(0, 0)
         u_passes(0, 1)
+        quantise_b(1)
+        turn_b(2)
+        turn_gates()
+        quantise_x(2)
+        part_b(3)
         u_passes(1, 0)
         u_passes(1, 1)
-        part_b(3)
         turn_x(3)
-        bias_cols(1)
         turn_b(3)
-        turn_gates()
         quantise_b(2)
         part_w(0)
         part_w(1)
-        quantise_x(3)
         u_passes(2, 0)
         u_passes(2, 1)
         u_passes(0, 2)
         u_passes(1, 2)
         u_passes(2, 2)
-        turn_w(0)
         quantise_b(3)
+        turn_w(0, ALL)
+        quantise_x(3)
         part_w(2)
         part_w(3)
         u_passes(3, 0)
         u_passes(3, 1)
         u_passes(3, 2)
         u_passes(0, 3)
-        h_block(0)
-        part_w(4)
-        turn_w(1)
-        quantise_w(0, (0, 1))
-        h_block(1)
-        part_w(5)
-        quantise_w(0, (2, 3))
         u_passes(1, 3)
+        part_w(4)
+        h_block(0)
+        turn_w(1, ALL)
+        quantise_w(0, LOW)
+        part_w(5)
+        quantise_w(0, HIGH)
         u_passes(2, 3)
         u_passes(3, 3)
+        h_block(1)
+        quantise_w(1, LOW)
+        turn_w(2, LOW)
+        sort_a(0, 0)
+        turn_w(2, HIGH)
+        quantise_w(1, HIGH)
+        sort_a(0, 1)
         h_block(2)
-        quantise_w(1, (0, 1, 2, 3))
         h_block(3)
-        quantise_h()
-        turn_w(2)
         base(0, 0)
         base(0, 1)
-        base(0, 2)
-        sort_a(0, 0)
-        sort_a(0, 1)
-        quantise_w(2, (0, 1, 2, 3))
+        quantise_w(2, LOW)
+        quantise_h()
         part_w(6)
         part_w(7)
         turn_a(0)
-        base(0, 3)
-        turn_w(3)
+        base(0, 2)
+        turn_w(3, ALL)
         part_w(8)
         quantise_a(0)
-        part_w(9)
+        base(0, 3)
         delta(0, 0)
         delta(0, 1)
         delta(0, 2)
+        part_w(9)
         sort_a(1, 0)
-        quantise_w(3, (0, 1, 2, 3))
+        turn_w(4, ALL)
+        quantise_w(2, HIGH)
+        quantise_w(3, ALL)
         finish(0, 0)
         sort_a(1, 1)
-        finish(0, 1)
-        turn_w(4)
         delta(0, 3)
-        base(1, 0)
-        delta(1, 0)
         part_w(10)
+        finish(0, 1)
         part_w(11)
         finish(0, 2)
-        quantise_w(4, (0, 1, 2, 3))
+        quantise_w(4, ALL)
+        base(1, 0)
+        delta(1, 0)
         finish(0, 3)
         turn_a(1)
-        base(1, 1)
-        delta(1, 1)
-        finish(1, 0)
         part_w(12)
+        base(1, 1)
+        turn_w(5, ALL)
         part_w(13)
-        quantise_a(1)
-        turn_w(5)
-        finish(1, 1)
+        quantise_w(5, ALL)
         base(1, 2)
-        delta(1, 2)
+        delta(1, 1)
         part_w(14)
-        quantise_w(5, (0, 1, 2, 3))
         part_w(15)
-        turn_w(6)
-        finish(1, 2)
-        quantise_w(6, (0, 1, 2, 3))
+        finish(1, 0)
+        quantise_a(1)
+        turn_w(6, ALL)
         base(1, 3)
-        delta(1, 3)
+        delta(1, 2)
+        finish(1, 1)
+        quantise_w(6, ALL)
+        turn_w(7, ALL)
         base(2, 0)
+        delta(1, 3)
         delta(2, 0)
-        turn_w(7)
+        finish(1, 2)
+        quantise_w(7, ALL)
         finish(1, 3)
-        quantise_w(7, (0, 1, 2, 3))
-        finish(2, 0)
         base(2, 1)
         delta(2, 1)
-        finish(2, 1)
+        finish(2, 0)
         base(2, 2)
         delta(2, 2)
-        finish(2, 2)
+        finish(2, 1)
         base(2, 3)
         delta(2, 3)
+        finish(2, 2)
         finish(2, 3)
         base(3, 0)
         delta(3, 0)

@@ -65,7 +65,7 @@ def tile_submatrixlinear_pa_kernel(tc, x, scores, Wb, bb, A, B, out):
         ones = const.tile([P, P], BF16, name="ones")
         nc.vector.memset(ones[:], 1.0)
         zeros = const.tile([P, 512], BF16, name="zeros")
-        nc.vector.memset(zeros[:], 0.0)
+        nc.gpsimd.memset(zeros[:].bitcast(F32), 0.0)
         bias_row = const.tile([P, D_OUT], BF16, name="bias_row")
         nc.vector.memset(bias_row[:], 0.0)
 
@@ -152,8 +152,8 @@ def tile_submatrixlinear_pa_kernel(tc, x, scores, Wb, bb, A, B, out):
         def part(src):
             t = work.tile([P, D_IN], BF16, name="parted", tag="parted", bufs=4)
             nc.vector.tensor_copy(
-                out=t[:].bitcast(F32).rearrange("q (g u p) -> q g u p", g=G, u=2),
-                in_=src[:].bitcast(F32).rearrange("q (g p u) -> q g u p", g=G, u=2),
+                out=t[:].bitcast(F32).rearrange("q (u c i) -> q c u i", u=2, i=4),
+                in_=src[:].bitcast(F32).rearrange("q (c i u) -> q c u i", i=4, u=2),
             )
             return t
 
@@ -166,7 +166,8 @@ def tile_submatrixlinear_pa_kernel(tc, x, scores, Wb, bb, A, B, out):
                 for g2 in range(2):
                     for u in range(2):
                         c0 = 256 * (2 * gp + g2)
-                        cols = slice(c0 + P * u, c0 + P * u + P) if parted else slice(c0 + u, c0 + 256, 2)
+                        p0 = 512 * u + P * (2 * gp + g2)
+                        cols = slice(p0, p0 + P) if parted else slice(c0 + u, c0 + 256, 2)
                         nc.tensor.transpose(bank[:, 2 * g2 + u, :], words[:, cols], ident[:])
                 nc.scalar.copy(out=dst[:, 2 * gp : 2 * gp + 2], in_=bank[:].rearrange("p (g u) n -> p g n u", u=2))
             return gx
@@ -209,8 +210,8 @@ def tile_submatrixlinear_pa_kernel(tc, x, scores, Wb, bb, A, B, out):
                 bank = psum_bank()
                 for j in range(2):
                     for u in range(2):
-                        c0 = 256 * g
-                        cols = slice(c0 + P * u, c0 + P * u + P)
+                        c0 = 512 * u + P * g
+                        cols = slice(c0, c0 + P)
                         nc.tensor.transpose(bank[:, 2 * j + u, :], w_parted[2 * s + j][:].bitcast(F32)[:, cols], ident[:])
                 nc.scalar.copy(out=dst[:, g], in_=bank[:].rearrange("p (j u) n -> p j n u", u=2))
 
@@ -318,7 +319,7 @@ def tile_submatrixlinear_pa_kernel(tc, x, scores, Wb, bb, A, B, out):
         def dummies(n):
             for i in range(n):
                 pd = accs.tile([P, 512], F32, name="pd", tag="acc")
-                nc.tensor.matmul(out=pd[:], lhsT=ones[:], rhs=zeros[:], start=True, stop=True)
+                nc.tensor.matmul(out=pd[:], lhsT=zeros[:, 0:P], rhs=zeros[:], start=True, stop=True)
 
         def bias_cols(i):
             pb = tps.tile([P, 1024], BF16, name="pb", tag="tp")

from contextlib import ExitStack

import concourse.mybir as mybir
from concourse.masks import make_identity

F32 = mybir.dt.float32
BF16 = mybir.dt.bfloat16
U32 = mybir.dt.uint32
U8 = mybir.dt.uint8
FP8X4 = mybir.dt.float8_e4m3fn_x4
ALU = mybir.AluOpType
ACT = mybir.ActivationFunctionType
AX = mybir.AxisListType

P = 128
N_TOK = 512
D_IN = 2048
D_OUT = 2048
N_EXP = 16
RANK = 32
KR = N_EXP * RANK
NB = N_TOK // P
G = D_IN // 512
MC = D_OUT // 512
GATE_THRESHOLD = 0.05

ALL = (0, 1, 2, 3)
LOW = (0, 1)
HIGH = (2, 3)

FLOPS = 2 * N_TOK * D_IN * D_OUT + 2 * N_TOK * D_IN * KR + 2 * N_TOK * KR * D_OUT


def tile_submatrixlinear_pa_kernel(tc, x, scores, Wb, bb, A, B, out):
    nc = tc.nc
    with ExitStack() as ctx:
        const = ctx.enter_context(tc.tile_pool(name="const", bufs=1))
        raw = ctx.enter_context(tc.tile_pool(name="raw", bufs=11))
        work = ctx.enter_context(tc.tile_pool(name="work", bufs=3))
        outp = ctx.enter_context(tc.tile_pool(name="outp", bufs=4))
        tps = ctx.enter_context(tc.psum_pool(name="tps", bufs=4))
        accs = ctx.enter_context(tc.psum_pool(name="accs", bufs=4))
        ctx.enter_context(tc.manual_schedule())

        bias_sb = const.tile([P, D_OUT], BF16, name="bias_sb")
        gt = const.tile([P, NB, P], F32, name="gt")
        xq = const.tile([P, NB, G, P], U32, name="xq", align_bytes=64)
        xs = const.tile([P, NB, G, P], U8, name="xs", align_bytes=64)
        bq = const.tile([P, 4, G, P], U32, name="bq", align_bytes=64)
        bs = const.tile([P, 4, G, P], U8, name="bs", align_bytes=64)
        wq = const.tile([P, MC, G, 512], U32, name="wq", align_bytes=64)
        ws = const.tile([P, MC, G, 512], U8, name="ws", align_bytes=64)
        aq = const.tile([P, D_OUT], U32, name="aq", align_bytes=64)
        asc = const.tile([P, D_OUT], U8, name="asc", align_bytes=64)
        hq = const.tile([P, NB, P], U32, name="hq", align_bytes=64)
        hs = const.tile([P, NB, P], U8, name="hs", align_bytes=64)
        hg = const.tile([P, NB, P, 4], BF16, name="hg", align_bytes=64)

        xv = x.rearrange("(p c) i -> c p i", c=NB)
        outv = out.rearrange("(p c) o -> c p o", c=NB)
        Bv = B.rearrange("k r i -> (k r) i").rearrange("(p t) i -> t p i", t=4)

        sc_b = const.tile([P, NB, N_EXP], BF16, name="sc_b")
        nc.scalar.dma_start(out=sc_b[:], in_=scores.rearrange("(p c) k -> p c k", c=NB))
        ones = const.tile([P, P], BF16, name="ones")
        nc.vector.memset(ones[:], 1.0)
        zeros = const.tile([P, 512], BF16, name="zeros")
        nc.gpsimd.memset(zeros[:].bitcast(F32), 0.0)
        bias_row = const.tile([P, D_OUT], BF16, name="bias_row")
        nc.vector.memset(bias_row[:], 0.0)

        def load_rows(src, cuts=1):
            t = raw.tile([P, D_IN], BF16, name="rows", tag="raw")
            step = D_IN // cuts
            for c in range(cuts):
                nc.sync.dma_start(out=t[:, step * c : step * c + step], in_=src[:, step * c : step * c + step])
            return t

        def load_a(half):
            z = const.tile([P, N_EXP, 256], BF16, name="z0_%d" % half)
            nc.sync.dma_start(
                out=z[:], in_=A[:, 1024 * half : 1024 * half + 1024, :].rearrange("k (w b) r -> w k (b r)", b=8)
            )
            return z

        ident = const.tile([P, P], F32, name="ident")
        make_identity(nc, ident[:])

        x_raw = []
        b_raw = []
        for c in range(NB):
            x_raw.append(load_rows(xv[c], 2 if c == 0 else 1))
            b_raw.append(load_rows(Bv[c]))
            if c == 0:
                nc.sync.dma_start(out=bias_row[0:1, :], in_=bb.rearrange("(o n) -> o n", o=1))
        w_raw = []
        z0 = []
        for i in range(D_OUT // P):
            w_raw.append(load_rows(Wb[P * i : P * i + P, :]))
            if i in (5, 9):
                z0.append(load_a(len(z0)))

        mx = const.tile([P, NB], F32, name="mx")
        dif = const.tile([P, NB, N_EXP], F32, name="dif")
        ex = const.tile([P, NB, N_EXP], F32, name="ex")
        sm = const.tile([P, NB], F32, name="sm")
        keep = const.tile([P, NB, N_EXP], F32, name="keep")
        g1 = const.tile([P, NB, N_EXP], F32, name="g1")
        s1 = const.tile([P, NB], F32, name="s1")
        r1 = const.tile([P, NB], F32, name="r1")
        gexp = const.tile([P, NB, P], F32, name="gexp")

        def gates_a():
            nc.vector.tensor_reduce(out=mx[:], in_=sc_b[:], axis=AX.X, op=ALU.max)
            nc.gpsimd.tensor_tensor(
                out=dif[:], in0=sc_b[:], in1=mx[:].unsqueeze(2).to_broadcast([P, NB, N_EXP]), op=ALU.subtract
            )
            nc.scalar.activation(out=ex[:], in_=dif[:], func=ACT.Exp)

        def gates_b():
            nc.vector.tensor_reduce(out=sm[:], in_=ex[:], axis=AX.X, op=ALU.add)
            nc.vector.scalar_tensor_tensor(
                out=keep[:],
                in0=sm[:].unsqueeze(2).to_broadcast([P, NB, N_EXP]),
                scalar=GATE_THRESHOLD,
                in1=ex[:],
                op0=ALU.mult,
                op1=ALU.is_lt,
            )
            nc.gpsimd.tensor_tensor(out=g1[:], in0=ex[:], in1=keep[:], op=ALU.mult)

        def gates_c():
            nc.vector.tensor_reduce(out=s1[:], in_=g1[:], axis=AX.X, op=ALU.add)
            nc.vector.reciprocal(out=r1[:], in_=s1[:])
            for nb in range(NB):
                nc.gpsimd.tensor_scalar(
                    out=gexp[:, nb, :].rearrange("p (k j) -> p k j", j=8),
                    in0=g1[:, nb, :].unsqueeze(2).to_broadcast([P, N_EXP, 8]),
                    scalar1=r1[:, nb : nb + 1],
                    scalar2=0.0,
                    op0=ALU.mult,
                    op1=ALU.add,
                )

        x_turned, b_parted, b_turned, w_parted, w_turned = {}, {}, {}, {}, {}
        a_sorted, a_turned, ut, acc = {}, {}, {}, {}

        def psum_bank():
            bank = tps.tile([P, 4, P], F32, name="bank", tag="tp")
            return bank

        def part(src):
            t = work.tile([P, D_IN], BF16, name="parted", tag="parted", bufs=4)
            nc.vector.tensor_copy(
                out=t[:].bitcast(F32).rearrange("q (u c i) -> q c u i", u=2, i=4),
                in_=src[:].bitcast(F32).rearrange("q (c i u) -> q c u i", i=4, u=2),
            )
            return t

        def turn_block(src, parted):
            gx = work.tile([P, D_IN], BF16, name="gx", tag="gx", align_bytes=64)
            dst = gx[:].bitcast(F32).rearrange("p (g n u) -> p g n u", g=G, u=2)
            words = src[:].bitcast(F32)
            for gp in range(2):
                bank = psum_bank()
                for g2 in range(2):
                    for u in range(2):
                        c0 = 256 * (2 * gp + g2)
                        p0 = 512 * u + P * (2 * gp + g2)
                        cols = slice(p0, p0 + P) if parted else slice(c0 + u, c0 + 256, 2)
                        nc.tensor.transpose(bank[:, 2 * g2 + u, :], words[:, cols], ident[:])
                nc.scalar.copy(out=dst[:, 2 * gp : 2 * gp + 2], in_=bank[:].rearrange("p (g u) n -> p g n u", u=2))
            return gx

        def quantise_block(gx, codes, scales):
            nc.vector.quantize_mx(
                out=codes.rearrange("p g n -> p (g n)").bitcast(FP8X4),
                scales=scales.rearrange("p g n -> p (g n)"),
                in_=gx[:],
            )

        def u_passes(t, nb):
            if nb not in ut:
                ut[nb] = accs.tile([P, 4, P], F32, name="ut%d" % nb, tag="acc")
            for g in range(G):
                nc.tensor.matmul_mx(
                    out=ut[nb][:, t, :],
                    lhsT=bq[:, t, g, :].bitcast(FP8X4),
                    lhsT_scale=bs[:, t, g, :],
                    rhs=xq[:, nb, g, :].bitcast(FP8X4),
                    rhs_scale=xs[:, nb, g, :],
                    start=(g == 0),
                    stop=(g == G - 1),
                )

        def h_block(nb):
            nc.vector.tensor_tensor(
                out=hg[:, nb],
                in0=ut[nb][:].rearrange("p t n -> p n t"),
                in1=gt[:, nb].unsqueeze(2).to_broadcast([P, P, 4]),
                op=ALU.mult,
            )

        def turn_w(s, passes):
            if s not in w_turned:
                w_turned[s] = work.tile([P, 2 * D_IN], BF16, name="wg", tag="wg", align_bytes=64)
            wg = w_turned[s]
            dst = wg[:].bitcast(F32).rearrange("p (g j n u) -> p g j n u", g=G, j=2, u=2)
            for g in passes:
                bank = psum_bank()
                for j in range(2):
                    for u in range(2):
                        c0 = 512 * u + P * g
                        cols = slice(c0, c0 + P)
                        nc.tensor.transpose(bank[:, 2 * j + u, :], w_parted[2 * s + j][:].bitcast(F32)[:, cols], ident[:])
                nc.scalar.copy(out=dst[:, g], in_=bank[:].rearrange("p (j u) n -> p j n u", u=2))

        def quantise_w(s, passes):
            m, c0 = s // 2, 256 * (s % 2)
            for g in passes:
                nc.vector.quantize_mx(
                    out=wq[:, m, g, c0 : c0 + 256].bitcast(FP8X4),
                    scales=ws[:, m, g, c0 : c0 + 256],
                    in_=w_turned[s][:, 1024 * g : 1024 * g + 1024],
                )

        def sort_a(half, u):
            if half not in a_sorted:
                a_sorted[half] = work.tile([P, 4096], BF16, name="z1", tag="z1", bufs=1)
            z1 = a_sorted[half]
            zo = z1[:].bitcast(F32).rearrange("p (b u k j) -> p u b k j", b=8, u=2, k=N_EXP)
            zi = z0[half][:].rearrange("p k c -> p (k c)").bitcast(F32)
            zi = zi.rearrange("p (k b j u) -> p u b k j", k=N_EXP, b=8, u=2)
            copy = nc.scalar.copy if u == 0 else nc.vector.tensor_copy
            copy(out=zo[:, u], in_=zi[:, u])

        def turn_a(half):
            y = work.tile([P, 4096], BF16, name="y", tag="y", bufs=1, align_bytes=64)
            yw = y[:].bitcast(F32).rearrange("p (w h bu) -> p h w bu", w=P, h=4)
            zw = a_sorted[half][:].bitcast(F32)
            for h in range(4):
                bank = psum_bank()
                for i in range(4):
                    c0 = P * (4 * h + i)
                    nc.tensor.transpose(bank[:, i, :], zw[:, c0 : c0 + P], ident[:])
                nc.scalar.copy(out=yw[:, h], in_=bank[:].rearrange("p bu w -> p w bu"))
            a_turned[half] = y

        def quantise_a(half):
            for i in range(2):
                c0 = 1024 * half + 512 * i
                nc.vector.quantize_mx(
                    out=aq[:, c0 : c0 + 512].bitcast(FP8X4),
                    scales=asc[:, c0 : c0 + 512],
                    in_=a_turned[half][:, 2048 * i : 2048 * i + 2048],
                )


        def base(m, nb):
            t = accs.tile([P, 512], F32, name="acc", tag="acc")
            for g in range(G):
                nc.tensor.matmul_mx(
                    out=t[:],
                    lhsT=xq[:, nb, g, :].bitcast(FP8X4),
                    lhsT_scale=xs[:, nb, g, :],
                    rhs=wq[:, m, g, :].bitcast(FP8X4),
                    rhs_scale=ws[:, m, g, :],
                    start=(g == 0),
                    stop=False,
                )
            acc[m, nb] = t

        def delta(m, nb):
            nc.tensor.matmul_mx(
                out=acc[m, nb][:],
                lhsT=hq[:, nb, :].bitcast(FP8X4),
                lhsT_scale=hs[:, nb, :],
                rhs=aq[:, 512 * m : 512 * m + 512].bitcast(FP8X4),
                rhs_scale=asc[:, 512 * m : 512 * m + 512],
                start=False,
                stop=True,
            )

        def finish(m, nb):
            o = outp.tile([P, 512], F32, name="o", tag="o")
            nc.vector.tensor_tensor(
                out=o[:], in0=acc[m, nb][:], in1=bias_sb[:, 512 * m : 512 * m + 512], op=ALU.add
            )
            nc.sync.dma_start(out=outv[nb][:, 512 * m : 512 * m + 512], in_=o[:])

        def last_group(m, nb):
            for i in range(2):
                t = accs.tile([P, 256], F32, name="half", tag="acc")
                cols = slice(256 * i, 256 * i + 256)
                for g in range(G):
                    nc.tensor.matmul_mx(
                        out=t[:],
                        lhsT=xq[:, nb, g, :].bitcast(FP8X4),
                        lhsT_scale=xs[:, nb, g, :],
                        rhs=wq[:, m, g, cols].bitcast(FP8X4),
                        rhs_scale=ws[:, m, g, cols],
                        start=(g == 0),
                        stop=False,
                    )
                c0 = 512 * m + 256 * i
                nc.tensor.matmul_mx(
                    out=t[:],
                    lhsT=hq[:, nb, :].bitcast(FP8X4),
                    lhsT_scale=hs[:, nb, :],
                    rhs=aq[:, c0 : c0 + 256].bitcast(FP8X4),
                    rhs_scale=asc[:, c0 : c0 + 256],
                    start=False,
                    stop=True,
                )
                o = outp.tile([P, 512], F32, name="o", tag="o")
                nc.vector.tensor_tensor(out=o[:, 0:256], in0=t[:], in1=bias_sb[:, c0 : c0 + 256], op=ALU.add)
                nc.sync.dma_start(out=outv[nb][:, c0 : c0 + 256], in_=o[:, 0:256])

        def dummies(n):
            for i in range(n):
                pd = accs.tile([P, 512], F32, name="pd", tag="acc")
                nc.tensor.matmul(out=pd[:], lhsT=zeros[:, 0:P], rhs=zeros[:], start=True, stop=True)

        def bias_cols(i):
            pb = tps.tile([P, 1024], BF16, name="pb", tag="tp")
            for j in range(2):
                c0 = 1024 * i + 512 * j
                nc.tensor.matmul(
                    out=pb[:, 512 * j : 512 * j + 512], lhsT=ones[:], rhs=bias_row[:, c0 : c0 + 512], start=True, stop=True
                )
            nc.scalar.copy(out=bias_sb[:, 1024 * i : 1024 * i + 1024], in_=pb[:])

        def turn_x(c):
            x_turned[c] = turn_block(x_raw[c], False)

        def quantise_x(c):
            quantise_block(x_turned[c], xq[:, c], xs[:, c])

        def part_b(t):
            b_parted[t] = part(b_raw[t])

        def turn_b(t):
            b_turned[t] = turn_block(b_parted[t], True) if t in b_parted else turn_block(b_raw[t], False)

        def quantise_b(t):
            quantise_block(b_turned[t], bq[:, t], bs[:, t])

        def part_w(i):
            w_parted[i] = part(w_raw[i])

        def turn_gates():
            bank = psum_bank()
            for c in range(NB):
                nc.tensor.transpose(bank[:, c, :], gexp[:, c, :], ident[:])
            nc.scalar.copy(out=gt[:], in_=bank[:])

        def quantise_h():
            nc.vector.quantize_mx(
                out=hq[:].rearrange("p c n -> p (c n)").bitcast(FP8X4),
                scales=hs[:].rearrange("p c n -> p (c n)"),
                in_=hg[:].rearrange("p c n t -> p (c n t)"),
            )

        dummies(5)
        gates_a()
        turn_x(0)
        dummies(2)
        gates_b()
        turn_b(0)
        quantise_x(0)
        bias_cols(0)
        turn_x(1)
        turn_b(1)
        bias_cols(1)
        quantise_b(0)
        gates_c()
        quantise_x(1)
        part_b(2)
        turn_x(2)
        u_passes(0, 0)
        u_passes(0, 1)
        quantise_b(1)
        turn_b(2)
        turn_gates()
        quantise_x(2)
        part_b(3)
        u_passes(1, 0)
        u_passes(1, 1)
        turn_x(3)
        turn_b(3)
        quantise_b(2)
        part_w(0)
        part_w(1)
        u_passes(2, 0)
        u_passes(2, 1)
        u_passes(0, 2)
        u_passes(1, 2)
        u_passes(2, 2)
        quantise_b(3)
        turn_w(0, ALL)
        quantise_x(3)
        part_w(2)
        part_w(3)
        u_passes(3, 0)
        u_passes(3, 1)
        u_passes(3, 2)
        u_passes(0, 3)
        u_passes(1, 3)
        part_w(4)
        h_block(0)
        turn_w(1, ALL)
        quantise_w(0, LOW)
        part_w(5)
        quantise_w(0, HIGH)
        u_passes(2, 3)
        u_passes(3, 3)
        h_block(1)
        quantise_w(1, LOW)
        turn_w(2, LOW)
        sort_a(0, 0)
        turn_w(2, HIGH)
        quantise_w(1, HIGH)
        sort_a(0, 1)
        h_block(2)
        h_block(3)
        base(0, 0)
        base(0, 1)
        quantise_w(2, LOW)
        quantise_h()
        part_w(6)
        part_w(7)
        turn_a(0)
        base(0, 2)
        turn_w(3, ALL)
        part_w(8)
        quantise_a(0)
        base(0, 3)
        delta(0, 0)
        delta(0, 1)
        delta(0, 2)
        part_w(9)
        sort_a(1, 0)
        turn_w(4, ALL)
        quantise_w(2, HIGH)
        quantise_w(3, ALL)
        finish(0, 0)
        sort_a(1, 1)
        delta(0, 3)
        part_w(10)
        finish(0, 1)
        part_w(11)
        finish(0, 2)
        quantise_w(4, ALL)
        base(1, 0)
        delta(1, 0)
        finish(0, 3)
        turn_a(1)
        part_w(12)
        base(1, 1)
        turn_w(5, ALL)
        part_w(13)
        quantise_w(5, ALL)
        base(1, 2)
        delta(1, 1)
        part_w(14)
        part_w(15)
        finish(1, 0)
        quantise_a(1)
        turn_w(6, ALL)
        base(1, 3)
        delta(1, 2)
        finish(1, 1)
        quantise_w(6, ALL)
        turn_w(7, ALL)
        base(2, 0)
        delta(1, 3)
        delta(2, 0)
        finish(1, 2)
        quantise_w(7, ALL)
        finish(1, 3)
        base(2, 1)
        delta(2, 1)
        finish(2, 0)
        base(2, 2)
        delta(2, 2)
        finish(2, 1)
        base(2, 3)
        delta(2, 3)
        finish(2, 2)
        finish(2, 3)
        base(3, 0)
        delta(3, 0)
        finish(3, 0)
        base(3, 1)
        delta(3, 1)
        finish(3, 1)
        base(3, 2)
        delta(3, 2)
        finish(3, 2)
        last_group(3, 3)
